import numpy as np
import ml_dtypes


def mxq(x, axis, fmt="e4m3"):
    dtype, down = {"e4m3": (ml_dtypes.float8_e4m3fn, 7), "e5m2": (ml_dtypes.float8_e5m2, 14)}[fmt]
    v = np.moveaxis(np.asarray(x, np.float32).astype(ml_dtypes.bfloat16).astype(np.float64), axis, -1)
    blocks = v.reshape(v.shape[:-1] + (-1, 32))
    amax = np.abs(blocks).max(-1, keepdims=True)
    byte = np.maximum(np.where(amax > 0, np.frexp(amax)[1] - 1 + 127, 0) - down, 1)
    scale = np.exp2(byte - 127.0)
    codes = (blocks / scale).astype(np.float32).astype(dtype).astype(np.float64)
    return np.moveaxis((codes * scale).reshape(v.shape), -1, axis)


WIDE = False


def mx_kscale(k):
    if not WIDE:
        return np.ones(k)
    levels = np.array([10, -10, 5, -5, 0])
    if k % 512:
        return np.exp2(np.random.permutation(np.resize(levels, k // 32))).repeat(32)
    a = np.empty((k // 512, 16))
    for p in range(k // 512):
        a[p, :8] = np.random.permutation(np.resize(levels, 8))
        for g in range(8):
            far = levels[np.abs(levels - a[p, g]) >= 10]
            a[p, g + 8] = far[np.random.randint(len(far))]
    return np.exp2(a.ravel()).repeat(32)


BF16 = ml_dtypes.bfloat16


def bf(x):
    return np.asarray(x, np.float32).astype(BF16)


def f64(x):
    return np.asarray(x).astype(np.float64)


B, L, H, G, DEPTH = 64, 64, 512, 256, 3
EPS = 1e-5


def layernorm(v, g, b):
    mu = v.mean(-1, keepdims=True)
    var = np.square(v - mu).mean(-1, keepdims=True)
    return (v - mu) / np.sqrt(var + EPS) * g + b


def setup_inputs():
    s, t = mx_kscale(H), mx_kscale(H)
    return {"x_nodes": bf(np.random.standard_normal((B, L, H)) * s),
            "w1": bf(np.random.standard_normal((H, H)) / np.sqrt(H) / s[:, None]),
            "b1": bf(np.random.standard_normal(H) * 0.3),
            "gamma": bf((1.0 + 0.1 * np.random.standard_normal(H)) * t),
            "beta": bf(0.2 * np.random.standard_normal(H) * t),
            "w2": bf(np.random.standard_normal((H, G)) / np.sqrt(H) / t[:, None]),
            "b2": bf(np.random.standard_normal(G) * 0.3)}


def reference(x_nodes, w1, b1, gamma, beta, w2, b2):
    h = (mxq(f64(x_nodes), 2, "e4m3") @ mxq(f64(w1), 0, "e4m3")) + f64(b1)
    r = np.maximum(layernorm(h, f64(gamma), f64(beta)), 0.0)
    x1 = (mxq(r, 2, "e4m3") @ mxq(f64(w2), 0, "e4m3")) + f64(b2)
    x2 = np.broadcast_to(x1.max(axis=1, keepdims=True), x1.shape)
    x = np.concatenate([x1, x2], axis=2)
    return x.max(axis=1)

@@ -1,0 +1,339 @@
+from contextlib import ExitStack
+
+import concourse.masks as masks
+import concourse.mybir as mybir
+
+F32 = mybir.dt.float32
+BF16 = mybir.dt.bfloat16
+U32 = mybir.dt.uint32
+U8 = mybir.dt.uint8
+FP8X4 = mybir.dt.float8_e4m3fn_x4
+ALU = mybir.AluOpType
+ACT = mybir.ActivationFunctionType
+AXIS = mybir.AxisListType
+
+P = 128
+PACK = 4
+POLYLINES = 64
+NODES = 64
+H = 512
+G = 256
+EPS = 1e-5
+TOKENS = POLYLINES * NODES
+TILES = 2
+UNIT = TILES * P
+UNITS = TOKENS // UNIT
+H_CHUNKS = H // P
+G_CHUNKS = G // P
+LINES_PER_UNIT = UNIT // NODES
+WORDS = H // 2
+LAST_LAG = 8
+RUN = 4
+
+FLOPS = 2 * TOKENS * H * H + 2 * TOKENS * H * G
+
+
+def group_words(copy, grouped, planes):
+    copy(
+        out=grouped[:].rearrange("p (c i) t -> p c t i", i=RUN),
+        in_=planes[:].rearrange("p t (c i) -> p c t i", i=RUN),
+    )
+
+
+def quantise(nc, codes, scales, grouped):
+    nc.vector.quantize_mx(
+        out=codes[:].bitcast(FP8X4),
+        scales=scales[:],
+        in_=grouped[:].rearrange("p c t -> p (c t)"),
+    )
+
+
+def tile_sub_graph_pb_kernel(tc, x_nodes, w1, b1, gamma, beta, w2, b2, out):
+    nc = tc.nc
+    x_flat = x_nodes.rearrange("b l k -> (b l) k")
+
+    with ExitStack() as ctx:
+        ctx.enter_context(tc.manual_schedule())
+        const = ctx.enter_context(tc.tile_pool(name="const", bufs=1))
+        x_pool = ctx.enter_context(tc.tile_pool(name="x", bufs=UNITS))
+        two = ctx.enter_context(tc.tile_pool(name="two", bufs=2))
+        three = ctx.enter_context(tc.tile_pool(name="three", bufs=3))
+        psum_x = ctx.enter_context(tc.psum_pool(name="psum_x", bufs=1))
+        psum_h = ctx.enter_context(tc.psum_pool(name="psum_h", bufs=2 * TILES))
+        psum_z = ctx.enter_context(tc.psum_pool(name="psum_z", bufs=2))
+        psum_x1 = ctx.enter_context(tc.psum_pool(name="psum_x1", bufs=1))
+
+        x_sb = {}
+
+        def load_x(unit):
+            x_sb[unit] = x_pool.tile([P, TILES * H], BF16, name="x_sb")
+            nc.sync.dma_start(
+                out=x_sb[unit][:].rearrange("p (i k) -> p i k", i=TILES),
+                in_=x_flat[unit * UNIT : (unit + 1) * UNIT, :].rearrange("(i p) k -> p i k", p=P),
+            )
+
+        load_x(0)
+        w1_raw = const.tile([P, PACK, H], BF16)
+        nc.scalar.dma_start(out=w1_raw[:], in_=w1.rearrange("(p j) c -> p j c", j=PACK))
+        load_x(1)
+        b1_row = const.tile([P, H], BF16)
+        nc.vector.memset(b1_row[:], 0.0)
+        nc.scalar.dma_start(out=b1_row[0:1, :], in_=b1.rearrange("(o c) -> o c", o=1))
+        rows_bf = const.tile([P, P], BF16)
+        nc.vector.memset(rows_bf[:], 0.0)
+        nc.scalar.dma_start(out=rows_bf[0:2, :], in_=b2.rearrange("(t p) -> t p", p=P))
+        gamma_bf = const.tile([P, PACK], BF16)
+        nc.scalar.dma_start(out=gamma_bf[:], in_=gamma.rearrange("(p t) -> p t", t=PACK))
+        beta_bf = const.tile([P, PACK], BF16)
+        nc.scalar.dma_start(out=beta_bf[:], in_=beta.rearrange("(p t) -> p t", t=PACK))
+        eps_col = const.tile([P, 1], F32)
+        nc.vector.memset(eps_col[:], EPS)
+        warm = const.tile([P, 1], F32)
+        nc.scalar.activation(out=warm[:], in_=eps_col[:], func=ACT.Sqrt)
+        w2_raw = const.tile([P, PACK, G], BF16)
+        nc.scalar.dma_start(out=w2_raw[:], in_=w2.rearrange("(p j) c -> p j c", j=PACK))
+        for unit in range(2, UNITS):
+            load_x(unit)
+
+        ident = const.tile([P, P], F32)
+        masks.make_identity(nc, ident[:])
+        ones = const.tile([P, P], BF16)
+        nc.vector.memset(ones[:], 1.0)
+        best = const.tile([P, G_CHUNKS, P], F32)
+        nc.vector.memset(best[:], 0.0)
+        b1_all = const.tile([P, H], F32)
+        gamma_cols = const.tile([P, PACK], F32)
+        beta_cols = const.tile([P, PACK], F32)
+        b2_cols = const.tile([P, G_CHUNKS], F32)
+
+        w1_grouped = const.tile([P, H, PACK], BF16, align_bytes=64)
+        w1_codes = const.tile([P, H], U32, align_bytes=64)
+        w1_scales = const.tile([P, H], U8, align_bytes=64)
+        w2_grouped = const.tile([P, G, PACK], BF16, align_bytes=64)
+        w2_codes = const.tile([P, G], U32, align_bytes=64)
+        w2_scales = const.tile([P, G], U8, align_bytes=64)
+
+        def spread_b1():
+            b1_ps = psum_z.tile([P, H], F32, tag="zT")
+            nc.tensor.matmul(out=b1_ps[:], lhsT=ones[:], rhs=b1_row[:], start=True, stop=True)
+            nc.scalar.copy(
+                out=b1_all[:].rearrange("p (t m) -> p t m", t=PACK),
+                in_=b1_ps[:].rearrange("p (m t) -> p t m", t=PACK),
+            )
+
+        def turn_vectors():
+            nc.scalar.copy(out=gamma_cols[:], in_=gamma_bf[:])
+            nc.scalar.copy(out=beta_cols[:], in_=beta_bf[:])
+            rows_f32 = const.tile([P, P], F32)
+            nc.scalar.copy(out=rows_f32[:], in_=rows_bf[:])
+            cols_ps = psum_z.tile([P, P], F32, tag="zT")
+            nc.tensor.transpose(out=cols_ps[:], in_=rows_f32[:], identity=ident[:])
+            nc.scalar.copy(out=b2_cols[:], in_=cols_ps[:, 0:G_CHUNKS])
+
+        kept = {}
+
+        def transpose_x(unit):
+            x_words = x_sb[unit][:].bitcast(F32)
+            xT = psum_x.tile([P, 2, UNIT], F32, tag="xT")
+            for i in range(TILES):
+                for u in range(2):
+                    nc.tensor.transpose(
+                        out=xT[:, u, i * P : (i + 1) * P],
+                        in_=x_words[:, WORDS * i + u : WORDS * (i + 1) : 2],
+                        identity=ident[:],
+                    )
+            kept["xT", unit] = xT
+
+        def group_x(unit):
+            x_grouped = two.tile([P, UNIT, PACK], BF16, align_bytes=64)
+            nc.scalar.copy(
+                out=x_grouped[:].rearrange("p c t -> p (c t)").bitcast(F32).rearrange("p (c u) -> p c u", u=2),
+                in_=kept["xT", unit][:].rearrange("p u c -> p c u"),
+            )
+            kept["x_grouped", unit] = x_grouped
+
+        def quantise_x(unit):
+            x_codes = two.tile([P, UNIT], U32, align_bytes=64)
+            x_scales = two.tile([P, UNIT], U8, align_bytes=64)
+            quantise(nc, x_codes, x_scales, kept["x_grouped", unit])
+            kept["x_codes", unit] = x_codes
+            kept["x_scales", unit] = x_scales
+
+        def multiply_w1(unit):
+            for i in range(TILES):
+                h_ps = psum_h.tile([P, H], F32, tag="h_ps")
+                nc.tensor.matmul_mx(
+                    out=h_ps[:],
+                    lhsT=kept["x_codes", unit][:, i * P : (i + 1) * P].bitcast(FP8X4),
+                    lhsT_scale=kept["x_scales", unit][:, i * P : (i + 1) * P],
+                    rhs=w1_codes[:].bitcast(FP8X4),
+                    rhs_scale=w1_scales[:],
+                    start=True,
+                    stop=True,
+                )
+                kept["h_ps", unit, i] = h_ps
+
+        def add_b1(unit):
+            h = three.tile([P, TILES, H], F32)
+            h_sum = two.tile([P, TILES], F32)
+            for i in range(TILES):
+                nc.vector.scalar_tensor_tensor(
+                    out=h[:, i, :],
+                    in0=kept["h_ps", unit, i][:],
+                    scalar=1.0,
+                    in1=b1_all[:],
+                    op0=ALU.mult,
+                    op1=ALU.add,
+                    accum_out=h_sum[:, i : i + 1],
+                )
+            kept["h", unit] = h
+            kept["h_sum", unit] = h_sum
+
+        def negate_mean(unit):
+            neg_mean = three.tile([P, TILES], F32)
+            nc.vector.tensor_scalar_mul(out=neg_mean[:], in0=kept["h_sum", unit][:], scalar1=-1.0 / H)
+            kept["neg_mean", unit] = neg_mean
+
+        def sum_squares(unit):
+            sq_sum = two.tile([P, TILES], F32)
+            for i in range(TILES):
+                squares = two.tile([P, H], BF16)
+                nc.scalar.activation(
+                    out=squares[:],
+                    in_=kept["h", unit][:, i, :],
+                    func=ACT.Square,
+                    bias=kept["neg_mean", unit][:, i : i + 1],
+                    accum_out=sq_sum[:, i : i + 1],
+                )
+            kept["sq_sum", unit] = sq_sum
+
+        def take_root(unit):
+            std = two.tile([P, TILES], F32)
+            nc.scalar.activation(
+                out=std[:], in_=kept["sq_sum", unit][:], func=ACT.Sqrt, bias=eps_col[:], scale=1.0 / H
+            )
+            kept["std", unit] = std
+
+        def invert_std(unit):
+            inv_std = two.tile([P, TILES], F32)
+            nc.vector.reciprocal(out=inv_std[:], in_=kept["std", unit][:])
+            kept["inv_std", unit] = inv_std
+
+        def normalise(unit):
+            z = two.tile([P, TILES, H], F32)
+            for i in range(TILES):
+                nc.gpsimd.tensor_scalar(
+                    out=z[:, i, :],
+                    in0=kept["h", unit][:, i, :],
+                    scalar1=kept["neg_mean", unit][:, i : i + 1],
+                    scalar2=kept["inv_std", unit][:, i : i + 1],
+                    op0=ALU.add,
+                    op1=ALU.mult,
+                )
+            kept["z", unit] = z
+
+        def transpose_z(unit):
+            for bank in range(2):
+                zT = psum_z.tile([P, 2, UNIT], F32, tag="zT")
+                for s in range(2):
+                    t = 2 * bank + s
+                    for i in range(TILES):
+                        nc.tensor.transpose(
+                            out=zT[:, s, i * P : (i + 1) * P],
+                            in_=kept["z", unit][:, i, t * P : (t + 1) * P],
+                            identity=ident[:],
+                        )
+                kept["zT", unit, bank] = zT
+
+        def scale_relu(unit):
+            r_planes = two.tile([P, H_CHUNKS, UNIT], BF16)
+            for t in range(H_CHUNKS):
+                nc.scalar.activation(
+                    out=r_planes[:, t, :],
+                    in_=kept["zT", unit, t // 2][:, t % 2, :],
+                    func=ACT.Relu,
+                    bias=beta_cols[:, t : t + 1],
+                    scale=gamma_cols[:, t : t + 1],
+                )
+            kept["r_planes", unit] = r_planes
+
+        def group_r(unit):
+            r_grouped = two.tile([P, UNIT, PACK], BF16, align_bytes=64)
+            group_words(nc.vector.tensor_copy, r_grouped, kept["r_planes", unit])
+            kept["r_grouped", unit] = r_grouped
+
+        def quantise_r(unit):
+            r_codes = two.tile([P, UNIT], U32, align_bytes=64)
+            r_scales = two.tile([P, UNIT], U8, align_bytes=64)
+            quantise(nc, r_codes, r_scales, kept["r_grouped", unit])
+            kept["r_codes", unit] = r_codes
+            kept["r_scales", unit] = r_scales
+
+        def multiply_w2(unit):
+            x1_ps = psum_x1.tile([P, G_CHUNKS, UNIT], F32, tag="x1_ps")
+            for c in range(G_CHUNKS):
+                nc.tensor.matmul_mx(
+                    out=x1_ps[:, c, :],
+                    lhsT=w2_codes[:, c * P : (c + 1) * P].bitcast(FP8X4),
+                    lhsT_scale=w2_scales[:, c * P : (c + 1) * P],
+                    rhs=kept["r_codes", unit][:].bitcast(FP8X4),
+                    rhs_scale=kept["r_scales", unit][:],
+                    start=True,
+                    stop=True,
+                )
+            kept["x1_ps", unit] = x1_ps
+
+        def take_max(unit):
+            nc.vector.tensor_reduce(
+                out=best[:, :, unit * LINES_PER_UNIT : (unit + 1) * LINES_PER_UNIT],
+                in_=kept["x1_ps", unit][:].rearrange("m c (b l) -> m c b l", l=NODES),
+                axis=AXIS.X,
+                op=ALU.max,
+            )
+
+        def at(step, unit):
+            if 0 <= unit < UNITS:
+                step(unit)
+
+        transpose_x(0)
+        for now in range(UNITS + LAST_LAG):
+            at(multiply_w1, now - 1)
+            at(invert_std, now - 4)
+            at(normalise, now - 4)
+            at(sum_squares, now - 3)
+            at(group_x, now)
+            at(take_root, now - 3)
+            if now == 0:
+                spread_b1()
+                nc.vector.tensor_copy(
+                    out=w1_grouped[:].rearrange("p (t m) j -> p t m j", t=PACK),
+                    in_=w1_raw[:].rearrange("p j (m t) -> p t m j", t=PACK),
+                )
+            at(add_b1, now - 2)
+            at(take_max, now - 8)
+            at(negate_mean, now - 2)
+            at(transpose_z, now - 5)
+            at(scale_relu, now - 5)
+            at(group_r, now - 6)
+            at(quantise_x, now)
+            if now == 0:
+                quantise(nc, w1_codes, w1_scales, w1_grouped)
+            at(quantise_r, now - 6)
+            at(transpose_x, now + 1)
+            at(multiply_w2, now - 7)
+            if now == 1:
+                group_words(nc.scalar.copy, w2_grouped, w2_raw)
+                turn_vectors()
+            if now == 2:
+                quantise(nc, w2_codes, w2_scales, w2_grouped)
+
+        outT = psum_x.tile([P, G_CHUNKS, P], F32, tag="xT")
+        for c in range(G_CHUNKS):
+            nc.vector.tensor_scalar_add(
+                out=best[:, c, 0:POLYLINES], in0=best[:, c, 0:POLYLINES], scalar1=b2_cols[:, c : c + 1]
+            )
+            nc.tensor.transpose(out=outT[:, c, :], in_=best[:, c, :], identity=ident[:])
+        out_sb = const.tile([P, G], F32)
+        nc.vector.tensor_copy(out=out_sb[:], in_=outT[:].rearrange("b c m -> b (c m)"))
+        nc.sync.dma_start(out=out[:, 0:G], in_=out_sb[0:POLYLINES, :])
+        nc.sync.dma_start(out=out[:, G : 2 * G], in_=out_sb[0:POLYLINES, :])

@@ -79,17 +79,17 @@ def tile_sub_graph_pb_kernel(tc, x_nodes, w1, b1, gamma, beta, w2, b2, out):
         b1_row = const.tile([P, H], BF16)
         nc.vector.memset(b1_row[:], 0.0)
         nc.scalar.dma_start(out=b1_row[0:1, :], in_=b1.rearrange("(o c) -> o c", o=1))
-        rows_bf = const.tile([P, P], BF16)
-        nc.vector.memset(rows_bf[:], 0.0)
-        nc.scalar.dma_start(out=rows_bf[0:2, :], in_=b2.rearrange("(t p) -> t p", p=P))
+        b2_row = const.tile([P, G], BF16)
+        nc.vector.memset(b2_row[:], 0.0)
+        nc.scalar.dma_start(out=b2_row[0:1, :], in_=b2.rearrange("(o c) -> o c", o=1))
         gamma_bf = const.tile([P, PACK], BF16)
         nc.scalar.dma_start(out=gamma_bf[:], in_=gamma.rearrange("(p t) -> p t", t=PACK))
         beta_bf = const.tile([P, PACK], BF16)
         nc.scalar.dma_start(out=beta_bf[:], in_=beta.rearrange("(p t) -> p t", t=PACK))
         eps_col = const.tile([P, 1], F32)
-        nc.vector.memset(eps_col[:], EPS)
+        nc.vector.memset(eps_col[:], EPS / H**2)
         warm = const.tile([P, 1], F32)
-        nc.scalar.activation(out=warm[:], in_=eps_col[:], func=ACT.Sqrt)
+        nc.scalar.activation(out=warm[:], in_=eps_col[:], func=ACT.Abs_reciprocal_sqrt)
         w2_raw = const.tile([P, PACK, G], BF16)
         nc.scalar.dma_start(out=w2_raw[:], in_=w2.rearrange("(p j) c -> p j c", j=PACK))
         for unit in range(2, UNITS):
@@ -104,7 +104,7 @@ def tile_sub_graph_pb_kernel(tc, x_nodes, w1, b1, gamma, beta, w2, b2, out):
         b1_all = const.tile([P, H], F32)
         gamma_cols = const.tile([P, PACK], F32)
         beta_cols = const.tile([P, PACK], F32)
-        b2_cols = const.tile([P, G_CHUNKS], F32)
+        b2_all = const.tile([P, G], F32)
 
         w1_grouped = const.tile([P, H, PACK], BF16, align_bytes=64)
         w1_codes = const.tile([P, H], U32, align_bytes=64)
@@ -116,19 +116,18 @@ def tile_sub_graph_pb_kernel(tc, x_nodes, w1, b1, gamma, beta, w2, b2, out):
         def spread_b1():
             b1_ps = psum_z.tile([P, H], F32, tag="zT")
             nc.tensor.matmul(out=b1_ps[:], lhsT=ones[:], rhs=b1_row[:], start=True, stop=True)
-            nc.scalar.copy(
-                out=b1_all[:].rearrange("p (t m) -> p t m", t=PACK),
-                in_=b1_ps[:].rearrange("p (m t) -> p t m", t=PACK),
+            nc.scalar.mul(
+                b1_all[:].rearrange("p (t m) -> p t m", t=PACK),
+                b1_ps[:].rearrange("p (m t) -> p t m", t=PACK),
+                1.0 / H,
             )
 
         def turn_vectors():
             nc.scalar.copy(out=gamma_cols[:], in_=gamma_bf[:])
             nc.scalar.copy(out=beta_cols[:], in_=beta_bf[:])
-            rows_f32 = const.tile([P, P], F32)
-            nc.scalar.copy(out=rows_f32[:], in_=rows_bf[:])
-            cols_ps = psum_z.tile([P, P], F32, tag="zT")
-            nc.tensor.transpose(out=cols_ps[:], in_=rows_f32[:], identity=ident[:])
-            nc.scalar.copy(out=b2_cols[:], in_=cols_ps[:, 0:G_CHUNKS])
+            b2_ps = psum_z.tile([P, G], F32, tag="zT")
+            nc.tensor.matmul(out=b2_ps[:], lhsT=ones[:], rhs=b2_row[:], start=True, stop=True)
+            nc.scalar.copy(out=b2_all[:], in_=b2_ps[:])
 
         kept = {}
 
@@ -175,24 +174,19 @@ def tile_sub_graph_pb_kernel(tc, x_nodes, w1, b1, gamma, beta, w2, b2, out):
 
         def add_b1(unit):
             h = three.tile([P, TILES, H], F32)
-            h_sum = two.tile([P, TILES], F32)
+            mean = three.tile([P, TILES], F32)
             for i in range(TILES):
                 nc.vector.scalar_tensor_tensor(
                     out=h[:, i, :],
                     in0=kept["h_ps", unit, i][:],
-                    scalar=1.0,
+                    scalar=1.0 / H,
                     in1=b1_all[:],
                     op0=ALU.mult,
                     op1=ALU.add,
-                    accum_out=h_sum[:, i : i + 1],
+                    accum_out=mean[:, i : i + 1],
                 )
             kept["h", unit] = h
-            kept["h_sum", unit] = h_sum
-
-        def negate_mean(unit):
-            neg_mean = three.tile([P, TILES], F32)
-            nc.vector.tensor_scalar_mul(out=neg_mean[:], in0=kept["h_sum", unit][:], scalar1=-1.0 / H)
-            kept["neg_mean", unit] = neg_mean
+            kept["mean", unit] = mean
 
         def sum_squares(unit):
             sq_sum = two.tile([P, TILES], F32)
@@ -202,22 +196,34 @@ def tile_sub_graph_pb_kernel(tc, x_nodes, w1, b1, gamma, beta, w2, b2, out):
                     out=squares[:],
                     in_=kept["h", unit][:, i, :],
                     func=ACT.Square,
-                    bias=kept["neg_mean", unit][:, i : i + 1],
+                    bias=kept["mean", unit][:, i : i + 1],
+                    scale=-float(H),
                     accum_out=sq_sum[:, i : i + 1],
                 )
             kept["sq_sum", unit] = sq_sum
 
         def take_root(unit):
-            std = two.tile([P, TILES], F32)
-            nc.scalar.activation(
-                out=std[:], in_=kept["sq_sum", unit][:], func=ACT.Sqrt, bias=eps_col[:], scale=1.0 / H
-            )
-            kept["std", unit] = std
-
-        def invert_std(unit):
             inv_std = two.tile([P, TILES], F32)
-            nc.vector.reciprocal(out=inv_std[:], in_=kept["std", unit][:])
+            nc.scalar.activation(
+                out=inv_std[:],
+                in_=kept["sq_sum", unit][:],
+                func=ACT.Abs_reciprocal_sqrt,
+                bias=eps_col[:],
+                scale=1.0 / H**3,
+            )
             kept["inv_std", unit] = inv_std
+
+        def scale_mean(unit):
+            shift = two.tile([P, TILES], F32)
+            nc.vector.scalar_tensor_tensor(
+                out=shift[:],
+                in0=kept["mean", unit][:],
+                scalar=-1.0 / H,
+                in1=kept["inv_std", unit][:],
+                op0=ALU.mult,
+                op1=ALU.mult,
+            )
+            kept["shift", unit] = shift
 
         def normalise(unit):
             z = two.tile([P, TILES, H], F32)
@@ -225,10 +231,10 @@ def tile_sub_graph_pb_kernel(tc, x_nodes, w1, b1, gamma, beta, w2, b2, out):
                 nc.gpsimd.tensor_scalar(
                     out=z[:, i, :],
                     in0=kept["h", unit][:, i, :],
-                    scalar1=kept["neg_mean", unit][:, i : i + 1],
-                    scalar2=kept["inv_std", unit][:, i : i + 1],
-                    op0=ALU.add,
-                    op1=ALU.mult,
+                    scalar1=kept["inv_std", unit][:, i : i + 1],
+                    scalar2=kept["shift", unit][:, i : i + 1],
+                    op0=ALU.mult,
+                    op1=ALU.add,
                 )
             kept["z", unit] = z
 
@@ -298,7 +304,7 @@ def tile_sub_graph_pb_kernel(tc, x_nodes, w1, b1, gamma, beta, w2, b2, out):
         transpose_x(0)
         for now in range(UNITS + LAST_LAG):
             at(multiply_w1, now - 1)
-            at(invert_std, now - 4)
+            at(scale_mean, now - 4)
             at(normalise, now - 4)
             at(sum_squares, now - 3)
             at(group_x, now)
@@ -311,7 +317,6 @@ def tile_sub_graph_pb_kernel(tc, x_nodes, w1, b1, gamma, beta, w2, b2, out):
                 )
             at(add_b1, now - 2)
             at(take_max, now - 8)
-            at(negate_mean, now - 2)
             at(transpose_z, now - 5)
             at(scale_relu, now - 5)
             at(group_r, now - 6)
@@ -329,11 +334,8 @@ def tile_sub_graph_pb_kernel(tc, x_nodes, w1, b1, gamma, beta, w2, b2, out):
 
         outT = psum_x.tile([P, G_CHUNKS, P], F32, tag="xT")
         for c in range(G_CHUNKS):
-            nc.vector.tensor_scalar_add(
-                out=best[:, c, 0:POLYLINES], in0=best[:, c, 0:POLYLINES], scalar1=b2_cols[:, c : c + 1]
-            )
             nc.tensor.transpose(out=outT[:, c, :], in_=best[:, c, :], identity=ident[:])
         out_sb = const.tile([P, G], F32)
-        nc.vector.tensor_copy(out=out_sb[:], in_=outT[:].rearrange("b c m -> b (c m)"))
+        nc.vector.tensor_add(out=out_sb[:], in0=outT[:].rearrange("b c m -> b (c m)"), in1=b2_all[:])
         nc.sync.dma_start(out=out[:, 0:G], in_=out_sb[0:POLYLINES, :])
-        nc.sync.dma_start(out=out[:, G : 2 * G], in_=out_sb[0:POLYLINES, :])
+        nc.scalar.dma_start(out=out[:, G : 2 * G], in_=out_sb[0:POLYLINES, :])

@@ -225,18 +225,18 @@ def tile_sub_graph_pb_kernel(tc, x_nodes, w1, b1, gamma, beta, w2, b2, out):
             )
             kept["shift", unit] = shift
 
-        def normalise(unit):
-            z = two.tile([P, TILES, H], F32)
-            for i in range(TILES):
-                nc.gpsimd.tensor_scalar(
-                    out=z[:, i, :],
-                    in0=kept["h", unit][:, i, :],
-                    scalar1=kept["inv_std", unit][:, i : i + 1],
-                    scalar2=kept["shift", unit][:, i : i + 1],
-                    op0=ALU.mult,
-                    op1=ALU.add,
-                )
-            kept["z", unit] = z
+        def normalise(engine, unit, i):
+            if i == 0:
+                kept["z", unit] = two.tile([P, TILES, H], F32, name="z")
+            z = kept["z", unit]
+            engine.tensor_scalar(
+                out=z[:, i, :],
+                in0=kept["h", unit][:, i, :],
+                scalar1=kept["inv_std", unit][:, i : i + 1],
+                scalar2=kept["shift", unit][:, i : i + 1],
+                op0=ALU.mult,
+                op1=ALU.add,
+            )
 
         def transpose_z(unit):
             for bank in range(2):
@@ -305,7 +305,7 @@ def tile_sub_graph_pb_kernel(tc, x_nodes, w1, b1, gamma, beta, w2, b2, out):
         for now in range(UNITS + LAST_LAG):
             at(multiply_w1, now - 1)
             at(scale_mean, now - 4)
-            at(normalise, now - 4)
+            at(lambda unit: normalise(nc.gpsimd, unit, 0), now - 4)
             at(sum_squares, now - 3)
             at(group_x, now)
             at(take_root, now - 3)
@@ -317,6 +317,7 @@ def tile_sub_graph_pb_kernel(tc, x_nodes, w1, b1, gamma, beta, w2, b2, out):
                 )
             at(add_b1, now - 2)
             at(take_max, now - 8)
+            at(lambda unit: normalise(nc.vector, unit, 1), now - 4)
             at(transpose_z, now - 5)
             at(scale_relu, now - 5)
             at(group_r, now - 6)

@@ -27,6 +27,7 @@ H_CHUNKS = H // P
 G_CHUNKS = G // P
 LINES_PER_UNIT = UNIT // NODES
 WORDS = H // 2
+VECTOR_GROUPS = 4
 LAST_LAG = 8
 RUN = 4
 
@@ -42,9 +43,9 @@ def group_words(copy, grouped, planes):
 
 def quantise(nc, codes, scales, grouped):
     nc.vector.quantize_mx(
-        out=codes[:].bitcast(FP8X4),
-        scales=scales[:],
-        in_=grouped[:].rearrange("p c t -> p (c t)"),
+        out=codes.bitcast(FP8X4),
+        scales=scales,
+        in_=grouped.rearrange("p c t -> p (c t)"),
     )
 
 
@@ -57,6 +58,7 @@ def tile_sub_graph_pb_kernel(tc, x_nodes, w1, b1, gamma, beta, w2, b2, out):
         const = ctx.enter_context(tc.tile_pool(name="const", bufs=1))
         x_pool = ctx.enter_context(tc.tile_pool(name="x", bufs=UNITS))
         two = ctx.enter_context(tc.tile_pool(name="two", bufs=2))
+        one = ctx.enter_context(tc.tile_pool(name="one", bufs=1))
         three = ctx.enter_context(tc.tile_pool(name="three", bufs=3))
         psum_x = ctx.enter_context(tc.psum_pool(name="psum_x", bufs=1))
         psum_h = ctx.enter_context(tc.psum_pool(name="psum_h", bufs=2 * TILES))
@@ -65,34 +67,41 @@ def tile_sub_graph_pb_kernel(tc, x_nodes, w1, b1, gamma, beta, w2, b2, out):
 
         x_sb = {}
 
-        def load_x(unit):
-            x_sb[unit] = x_pool.tile([P, TILES * H], BF16, name="x_sb")
+        def load_x(unit, tiles=range(TILES)):
+            if unit not in x_sb:
+                x_sb[unit] = x_pool.tile([P, TILES * H], BF16, name="x_sb")
+            first, count = tiles[0], len(tiles)
             nc.sync.dma_start(
-                out=x_sb[unit][:].rearrange("p (i k) -> p i k", i=TILES),
-                in_=x_flat[unit * UNIT : (unit + 1) * UNIT, :].rearrange("(i p) k -> p i k", p=P),
+                out=x_sb[unit][:, first * H : (first + count) * H].rearrange("p (i k) -> p i k", i=count),
+                in_=x_flat[unit * UNIT + first * P : unit * UNIT + (first + count) * P, :].rearrange(
+                    "(i p) k -> p i k", p=P
+                ),
             )
 
-        load_x(0)
-        w1_raw = const.tile([P, PACK, H], BF16)
-        nc.scalar.dma_start(out=w1_raw[:], in_=w1.rearrange("(p j) c -> p j c", j=PACK))
-        load_x(1)
-        b1_row = const.tile([P, H], BF16)
-        nc.vector.memset(b1_row[:], 0.0)
-        nc.scalar.dma_start(out=b1_row[0:1, :], in_=b1.rearrange("(o c) -> o c", o=1))
-        b2_row = const.tile([P, G], BF16)
-        nc.vector.memset(b2_row[:], 0.0)
-        nc.scalar.dma_start(out=b2_row[0:1, :], in_=b2.rearrange("(o c) -> o c", o=1))
-        gamma_bf = const.tile([P, PACK], BF16)
-        nc.scalar.dma_start(out=gamma_bf[:], in_=gamma.rearrange("(p t) -> p t", t=PACK))
-        beta_bf = const.tile([P, PACK], BF16)
-        nc.scalar.dma_start(out=beta_bf[:], in_=beta.rearrange("(p t) -> p t", t=PACK))
         eps_col = const.tile([P, 1], F32)
         nc.vector.memset(eps_col[:], EPS / H**2)
         warm = const.tile([P, 1], F32)
         nc.scalar.activation(out=warm[:], in_=eps_col[:], func=ACT.Abs_reciprocal_sqrt)
+        b1_row = const.tile([P, H], BF16)
+        nc.vector.memset(b1_row[:], 0.0)
+        b2_row = const.tile([P, G], BF16)
+        nc.vector.memset(b2_row[:], 0.0)
+
+        w1_raw = const.tile([P, PACK, H], BF16)
+        nc.sync.dma_start(out=w1_raw[:], in_=w1.rearrange("(p j) c -> p j c", j=PACK))
+        for i in range(TILES):
+            load_x(0, [i])
+        nc.sync.dma_start(out=b1_row[0:1, :], in_=b1.rearrange("(o c) -> o c", o=1))
+        load_x(1)
+        gamma_bf = const.tile([P, PACK], BF16)
+        nc.sync.dma_start(out=gamma_bf[:], in_=gamma.rearrange("(p t) -> p t", t=PACK))
+        beta_bf = const.tile([P, PACK], BF16)
+        nc.sync.dma_start(out=beta_bf[:], in_=beta.rearrange("(p t) -> p t", t=PACK))
+        load_x(2)
         w2_raw = const.tile([P, PACK, G], BF16)
-        nc.scalar.dma_start(out=w2_raw[:], in_=w2.rearrange("(p j) c -> p j c", j=PACK))
-        for unit in range(2, UNITS):
+        nc.sync.dma_start(out=w2_raw[:], in_=w2.rearrange("(p j) c -> p j c", j=PACK))
+        nc.sync.dma_start(out=b2_row[0:1, :], in_=b2.rearrange("(o c) -> o c", o=1))
+        for unit in range(3, UNITS):
             load_x(unit)
 
         ident = const.tile([P, P], F32)
@@ -113,6 +122,13 @@ def tile_sub_graph_pb_kernel(tc, x_nodes, w1, b1, gamma, beta, w2, b2, out):
         w2_codes = const.tile([P, G], U32, align_bytes=64)
         w2_scales = const.tile([P, G], U8, align_bytes=64)
 
+        def group_w1():
+            grouped = w1_grouped[:].rearrange("p (t m) j -> p t m j", t=PACK)
+            raw = w1_raw[:].rearrange("p j (m t) -> p t m j", t=PACK)
+            nc.scalar.copy(out=grouped[:, 3, :, :], in_=raw[:, 3, :, :])
+            nc.vector.tensor_copy(out=grouped[:, 0:2, :, :], in_=raw[:, 0:2, :, :])
+            nc.vector.tensor_copy(out=grouped[:, 2, :, :], in_=raw[:, 2, :, :])
+
         def spread_b1():
             b1_ps = psum_z.tile([P, H], F32, tag="zT")
             nc.tensor.matmul(out=b1_ps[:], lhsT=ones[:], rhs=b1_row[:], start=True, stop=True)
@@ -122,41 +138,54 @@ def tile_sub_graph_pb_kernel(tc, x_nodes, w1, b1, gamma, beta, w2, b2, out):
                 1.0 / H,
             )
 
-        def turn_vectors():
-            nc.scalar.copy(out=gamma_cols[:], in_=gamma_bf[:])
-            nc.scalar.copy(out=beta_cols[:], in_=beta_bf[:])
+        def widen_vectors():
+            nc.gpsimd.tensor_copy(out=gamma_cols[:], in_=gamma_bf[:])
+            nc.gpsimd.tensor_copy(out=beta_cols[:], in_=beta_bf[:])
+
+        def spread_b2():
             b2_ps = psum_z.tile([P, G], F32, tag="zT")
             nc.tensor.matmul(out=b2_ps[:], lhsT=ones[:], rhs=b2_row[:], start=True, stop=True)
             nc.scalar.copy(out=b2_all[:], in_=b2_ps[:])
 
         kept = {}
 
-        def transpose_x(unit):
+        def transpose_x(unit, tiles=range(TILES)):
             x_words = x_sb[unit][:].bitcast(F32)
-            xT = psum_x.tile([P, 2, UNIT], F32, tag="xT")
-            for i in range(TILES):
+            if tiles[0] == 0:
+                kept["xT", unit] = psum_x.tile([P, 2, UNIT], F32, tag="xT", name="xT")
+            xT = kept["xT", unit]
+            for i in tiles:
                 for u in range(2):
                     nc.tensor.transpose(
                         out=xT[:, u, i * P : (i + 1) * P],
                         in_=x_words[:, WORDS * i + u : WORDS * (i + 1) : 2],
                         identity=ident[:],
                     )
-            kept["xT", unit] = xT
 
-        def group_x(unit):
-            x_grouped = two.tile([P, UNIT, PACK], BF16, align_bytes=64)
+        def columns(tiles):
+            return slice(tiles[0] * P, (tiles[-1] + 1) * P)
+
+        def group_x(unit, tiles=range(TILES)):
+            if tiles[0] == 0:
+                kept["x_grouped", unit] = two.tile([P, UNIT, PACK], BF16, name="x_grouped", align_bytes=64)
             nc.scalar.copy(
-                out=x_grouped[:].rearrange("p c t -> p (c t)").bitcast(F32).rearrange("p (c u) -> p c u", u=2),
-                in_=kept["xT", unit][:].rearrange("p u c -> p c u"),
+                out=kept["x_grouped", unit][:]
+                .rearrange("p c t -> p (c t)")
+                .bitcast(F32)
+                .rearrange("p (c u) -> p c u", u=2)[:, columns(tiles), :],
+                in_=kept["xT", unit][:, :, columns(tiles)].rearrange("p u c -> p c u"),
             )
-            kept["x_grouped", unit] = x_grouped
 
-        def quantise_x(unit):
-            x_codes = two.tile([P, UNIT], U32, align_bytes=64)
-            x_scales = two.tile([P, UNIT], U8, align_bytes=64)
-            quantise(nc, x_codes, x_scales, kept["x_grouped", unit])
-            kept["x_codes", unit] = x_codes
-            kept["x_scales", unit] = x_scales
+        def quantise_x(unit, tiles=range(TILES)):
+            if tiles[0] == 0:
+                kept["x_codes", unit] = two.tile([P, UNIT], U32, name="x_codes", align_bytes=64)
+                kept["x_scales", unit] = two.tile([P, UNIT], U8, name="x_scales", align_bytes=64)
+            quantise(
+                nc,
+                kept["x_codes", unit][:, columns(tiles)],
+                kept["x_scales", unit][:, columns(tiles)],
+                kept["x_grouped", unit][:, columns(tiles), :],
+            )
 
         def multiply_w1(unit):
             for i in range(TILES):
@@ -238,6 +267,7 @@ def tile_sub_graph_pb_kernel(tc, x_nodes, w1, b1, gamma, beta, w2, b2, out):
                 op1=ALU.add,
             )
 
+
         def transpose_z(unit):
             for bank in range(2):
                 zT = psum_z.tile([P, 2, UNIT], F32, tag="zT")
@@ -264,14 +294,24 @@ def tile_sub_graph_pb_kernel(tc, x_nodes, w1, b1, gamma, beta, w2, b2, out):
             kept["r_planes", unit] = r_planes
 
         def group_r(unit):
-            r_grouped = two.tile([P, UNIT, PACK], BF16, align_bytes=64)
-            group_words(nc.vector.tensor_copy, r_grouped, kept["r_planes", unit])
+            r_grouped = one.tile([P, UNIT, PACK], BF16, align_bytes=64)
+            if unit >= UNITS - VECTOR_GROUPS:
+                group_words(nc.vector.tensor_copy, r_grouped, kept["r_planes", unit])
+            else:
+                nc.gpsimd.tensor_scalar(
+                    out=r_grouped[:].rearrange("p (c i) t -> p c t i", i=RUN),
+                    in0=kept["r_planes", unit][:].rearrange("p t (c i) -> p c t i", i=RUN),
+                    scalar1=1.0,
+                    scalar2=0.0,
+                    op0=ALU.mult,
+                    op1=ALU.max,
+                )
             kept["r_grouped", unit] = r_grouped
 
         def quantise_r(unit):
             r_codes = two.tile([P, UNIT], U32, align_bytes=64)
             r_scales = two.tile([P, UNIT], U8, align_bytes=64)
-            quantise(nc, r_codes, r_scales, kept["r_grouped", unit])
+            quantise(nc, r_codes[:], r_scales[:], kept["r_grouped", unit][:])
             kept["r_codes", unit] = r_codes
             kept["r_scales", unit] = r_scales
 
@@ -301,39 +341,42 @@ def tile_sub_graph_pb_kernel(tc, x_nodes, w1, b1, gamma, beta, w2, b2, out):
             if 0 <= unit < UNITS:
                 step(unit)
 
-        transpose_x(0)
-        for now in range(UNITS + LAST_LAG):
+        for i in range(TILES):
+            transpose_x(0, [i])
+        group_w1()
+        for i in range(TILES):
+            group_x(0, [i])
+        spread_b1()
+        quantise_x(0, [0])
+        quantise(nc, w1_codes[:], w1_scales[:], w1_grouped[:])
+        quantise_x(0, [1])
+        widen_vectors()
+        transpose_x(1)
+        for now in range(1, UNITS + LAST_LAG):
             at(multiply_w1, now - 1)
-            at(scale_mean, now - 4)
-            at(lambda unit: normalise(nc.gpsimd, unit, 0), now - 4)
             at(sum_squares, now - 3)
             at(group_x, now)
             at(take_root, now - 3)
-            if now == 0:
-                spread_b1()
-                nc.vector.tensor_copy(
-                    out=w1_grouped[:].rearrange("p (t m) j -> p t m j", t=PACK),
-                    in_=w1_raw[:].rearrange("p j (m t) -> p t m j", t=PACK),
-                )
+            at(group_r, now - 6)
             at(add_b1, now - 2)
             at(take_max, now - 8)
+            at(scale_mean, now - 4)
+            at(quantise_x, now)
+            at(lambda unit: normalise(nc.vector, unit, 0), now - 4)
             at(lambda unit: normalise(nc.vector, unit, 1), now - 4)
             at(transpose_z, now - 5)
             at(scale_relu, now - 5)
-            at(group_r, now - 6)
-            at(quantise_x, now)
-            if now == 0:
-                quantise(nc, w1_codes, w1_scales, w1_grouped)
             at(quantise_r, now - 6)
             at(transpose_x, now + 1)
             at(multiply_w2, now - 7)
-            if now == 1:
-                group_words(nc.scalar.copy, w2_grouped, w2_raw)
-                turn_vectors()
             if now == 2:
-                quantise(nc, w2_codes, w2_scales, w2_grouped)
+                group_words(nc.vector.tensor_copy, w2_grouped, w2_raw)
+            if now == 3:
+                quantise(nc, w2_codes[:], w2_scales[:], w2_grouped[:])
+            if now == 6:
+                spread_b2()
 
-        outT = psum_x.tile([P, G_CHUNKS, P], F32, tag="xT")
+        outT = psum_x.tile([P, G_CHUNKS, P], F32, name="outT", tag="xT")
         for c in range(G_CHUNKS):
             nc.tensor.transpose(out=outT[:, c, :], in_=best[:, c, :], identity=ident[:])
         out_sb = const.tile([P, G], F32)

@@ -282,7 +282,7 @@ def tile_sub_graph_pb_kernel(tc, x_nodes, w1, b1, gamma, beta, w2, b2, out):
                 kept["zT", unit, bank] = zT
 
         def scale_relu(unit):
-            r_planes = two.tile([P, H_CHUNKS, UNIT], BF16)
+            r_planes = three.tile([P, H_CHUNKS, UNIT], BF16)
             for t in range(H_CHUNKS):
                 nc.scalar.activation(
                     out=r_planes[:, t, :],
@@ -304,7 +304,7 @@ def tile_sub_graph_pb_kernel(tc, x_nodes, w1, b1, gamma, beta, w2, b2, out):
                     scalar1=1.0,
                     scalar2=0.0,
                     op0=ALU.mult,
-                    op1=ALU.max,
+                    op1=ALU.add,
                 )
             kept["r_grouped", unit] = r_grouped
 
@@ -357,13 +357,16 @@ def tile_sub_graph_pb_kernel(tc, x_nodes, w1, b1, gamma, beta, w2, b2, out):
             at(sum_squares, now - 3)
             at(group_x, now)
             at(take_root, now - 3)
-            at(group_r, now - 6)
+            if now < UNITS + 2:
+                at(group_r, now - 6)
             at(add_b1, now - 2)
             at(take_max, now - 8)
             at(scale_mean, now - 4)
             at(quantise_x, now)
             at(lambda unit: normalise(nc.vector, unit, 0), now - 4)
             at(lambda unit: normalise(nc.vector, unit, 1), now - 4)
+            if now >= UNITS + 2:
+                at(group_r, now - 6)
             at(transpose_z, now - 5)
             at(scale_relu, now - 5)
             at(quantise_r, now - 6)

@@ -28,7 +28,7 @@ G_CHUNKS = G // P
 LINES_PER_UNIT = UNIT // NODES
 WORDS = H // 2
 VECTOR_GROUPS = 4
-LAST_LAG = 8
+LAST_LAG = 7
 RUN = 4
 
 FLOPS = 2 * TOKENS * H * H + 2 * TOKENS * H * G
@@ -88,9 +88,9 @@ def tile_sub_graph_pb_kernel(tc, x_nodes, w1, b1, gamma, beta, w2, b2, out):
         nc.vector.memset(b2_row[:], 0.0)
 
         w1_raw = const.tile([P, PACK, H], BF16)
+        load_x(0, [0])
         nc.sync.dma_start(out=w1_raw[:], in_=w1.rearrange("(p j) c -> p j c", j=PACK))
-        for i in range(TILES):
-            load_x(0, [i])
+        load_x(0, [1])
         nc.sync.dma_start(out=b1_row[0:1, :], in_=b1.rearrange("(o c) -> o c", o=1))
         load_x(1)
         gamma_bf = const.tile([P, PACK], BF16)
@@ -122,6 +122,8 @@ def tile_sub_graph_pb_kernel(tc, x_nodes, w1, b1, gamma, beta, w2, b2, out):
         w2_codes = const.tile([P, G], U32, align_bytes=64)
         w2_scales = const.tile([P, G], U8, align_bytes=64)
 
+        kept = {}
+
         def group_w1():
             grouped = w1_grouped[:].rearrange("p (t m) j -> p t m j", t=PACK)
             raw = w1_raw[:].rearrange("p j (m t) -> p t m j", t=PACK)
@@ -131,33 +133,35 @@ def tile_sub_graph_pb_kernel(tc, x_nodes, w1, b1, gamma, beta, w2, b2, out):
 
         def spread_b1():
             b1_ps = psum_z.tile([P, H], F32, tag="zT")
+            kept["b1_ps"] = b1_ps
             nc.tensor.matmul(out=b1_ps[:], lhsT=ones[:], rhs=b1_row[:], start=True, stop=True)
-            nc.scalar.mul(
-                b1_all[:].rearrange("p (t m) -> p t m", t=PACK),
-                b1_ps[:].rearrange("p (m t) -> p t m", t=PACK),
-                1.0 / H,
+
+        def place_b1():
+            nc.vector.tensor_scalar_mul(
+                out=b1_all[:].rearrange("p (t m) -> p t m", t=PACK),
+                in0=kept["b1_ps"][:].rearrange("p (m t) -> p t m", t=PACK),
+                scalar1=1.0 / H,
             )
 
         def widen_vectors():
-            nc.gpsimd.tensor_copy(out=gamma_cols[:], in_=gamma_bf[:])
-            nc.gpsimd.tensor_copy(out=beta_cols[:], in_=beta_bf[:])
+            nc.vector.tensor_copy(out=gamma_cols[:], in_=gamma_bf[:])
+            nc.vector.tensor_copy(out=beta_cols[:], in_=beta_bf[:])
 
         def spread_b2():
             b2_ps = psum_z.tile([P, G], F32, tag="zT")
             nc.tensor.matmul(out=b2_ps[:], lhsT=ones[:], rhs=b2_row[:], start=True, stop=True)
-            nc.scalar.copy(out=b2_all[:], in_=b2_ps[:])
+            nc.vector.tensor_copy(out=b2_all[:], in_=b2_ps[:])
 
-        kept = {}
 
-        def transpose_x(unit, tiles=range(TILES)):
+        def transpose_x(unit, tiles=range(TILES), pool=psum_x, tag="xT"):
             x_words = x_sb[unit][:].bitcast(F32)
             if tiles[0] == 0:
-                kept["xT", unit] = psum_x.tile([P, 2, UNIT], F32, tag="xT", name="xT")
+                kept["xT", unit] = pool.tile([P, TILES, 2, P], F32, tag=tag, name="xT")
             xT = kept["xT", unit]
             for i in tiles:
                 for u in range(2):
                     nc.tensor.transpose(
-                        out=xT[:, u, i * P : (i + 1) * P],
+                        out=xT[:, i, u, :],
                         in_=x_words[:, WORDS * i + u : WORDS * (i + 1) : 2],
                         identity=ident[:],
                     )
@@ -172,14 +176,14 @@ def tile_sub_graph_pb_kernel(tc, x_nodes, w1, b1, gamma, beta, w2, b2, out):
                 out=kept["x_grouped", unit][:]
                 .rearrange("p c t -> p (c t)")
                 .bitcast(F32)
-                .rearrange("p (c u) -> p c u", u=2)[:, columns(tiles), :],
-                in_=kept["xT", unit][:, :, columns(tiles)].rearrange("p u c -> p c u"),
+                .rearrange("p (i c u) -> p i c u", i=TILES, u=2)[:, tiles[0] : tiles[-1] + 1, :, :],
+                in_=kept["xT", unit][:, tiles[0] : tiles[-1] + 1, :, :].rearrange("p i u c -> p i c u"),
             )
 
         def quantise_x(unit, tiles=range(TILES)):
             if tiles[0] == 0:
-                kept["x_codes", unit] = two.tile([P, UNIT], U32, name="x_codes", align_bytes=64)
-                kept["x_scales", unit] = two.tile([P, UNIT], U8, name="x_scales", align_bytes=64)
+                kept["x_codes", unit] = three.tile([P, UNIT], U32, name="x_codes", align_bytes=64)
+                kept["x_scales", unit] = three.tile([P, UNIT], U8, name="x_scales", align_bytes=64)
             quantise(
                 nc,
                 kept["x_codes", unit][:, columns(tiles)],
@@ -343,40 +347,45 @@ def tile_sub_graph_pb_kernel(tc, x_nodes, w1, b1, gamma, beta, w2, b2, out):
 
         for i in range(TILES):
             transpose_x(0, [i])
-        group_w1()
-        for i in range(TILES):
-            group_x(0, [i])
         spread_b1()
+        transpose_x(1, pool=psum_z, tag="zT")
+        group_x(0, [0])
+        group_w1()
+        group_x(0, [1])
+        group_x(1)
+        transpose_x(2)
         quantise_x(0, [0])
         quantise(nc, w1_codes[:], w1_scales[:], w1_grouped[:])
         quantise_x(0, [1])
-        widen_vectors()
-        transpose_x(1)
+        place_b1()
+        quantise_x(1)
+        multiply_w1(0)
         for now in range(1, UNITS + LAST_LAG):
-            at(multiply_w1, now - 1)
-            at(sum_squares, now - 3)
-            at(group_x, now)
-            at(take_root, now - 3)
-            if now < UNITS + 2:
-                at(group_r, now - 6)
-            at(add_b1, now - 2)
-            at(take_max, now - 8)
-            at(scale_mean, now - 4)
-            at(quantise_x, now)
-            at(lambda unit: normalise(nc.vector, unit, 0), now - 4)
-            at(lambda unit: normalise(nc.vector, unit, 1), now - 4)
-            if now >= UNITS + 2:
-                at(group_r, now - 6)
-            at(transpose_z, now - 5)
-            at(scale_relu, now - 5)
-            at(quantise_r, now - 6)
-            at(transpose_x, now + 1)
-            at(multiply_w2, now - 7)
-            if now == 2:
+            at(sum_squares, now - 2)
+            at(group_x, now + 1)
+            at(take_root, now - 2)
+            if now < UNITS + 1:
+                at(group_r, now - 5)
+            at(add_b1, now - 1)
+            at(take_max, now - 7)
+            at(scale_mean, now - 3)
+            at(quantise_x, now + 1)
+            if now >= UNITS + 1:
+                at(group_r, now - 5)
+            at(lambda unit: normalise(nc.vector, unit, 0), now - 3)
+            at(lambda unit: normalise(nc.vector, unit, 1), now - 3)
+            at(transpose_z, now - 4)
+            at(scale_relu, now - 4)
+            at(quantise_r, now - 5)
+            at(multiply_w2, now - 6)
+            at(multiply_w1, now)
+            at(transpose_x, now + 2)
+            if now == 1:
                 group_words(nc.vector.tensor_copy, w2_grouped, w2_raw)
-            if now == 3:
+            if now == 2:
+                widen_vectors()
                 quantise(nc, w2_codes[:], w2_scales[:], w2_grouped[:])
-            if now == 6:
+            if now == 5:
                 spread_b2()
 
         outT = psum_x.tile([P, G_CHUNKS, P], F32, name="outT", tag="xT")

@@ -58,6 +58,7 @@ def tile_sub_graph_pb_kernel(tc, x_nodes, w1, b1, gamma, beta, w2, b2, out):
         const = ctx.enter_context(tc.tile_pool(name="const", bufs=1))
         x_pool = ctx.enter_context(tc.tile_pool(name="x", bufs=UNITS))
         two = ctx.enter_context(tc.tile_pool(name="two", bufs=2))
+        every = ctx.enter_context(tc.tile_pool(name="every", bufs=UNITS))
         one = ctx.enter_context(tc.tile_pool(name="one", bufs=1))
         three = ctx.enter_context(tc.tile_pool(name="three", bufs=3))
         psum_x = ctx.enter_context(tc.psum_pool(name="psum_x", bufs=1))
@@ -206,8 +207,8 @@ def tile_sub_graph_pb_kernel(tc, x_nodes, w1, b1, gamma, beta, w2, b2, out):
                 kept["h_ps", unit, i] = h_ps
 
         def add_b1(unit):
-            h = three.tile([P, TILES, H], F32)
-            mean = three.tile([P, TILES], F32)
+            h = every.tile([P, TILES, H], F32)
+            mean = every.tile([P, TILES], F32)
             for i in range(TILES):
                 nc.vector.scalar_tensor_tensor(
                     out=h[:, i, :],
@@ -222,7 +223,7 @@ def tile_sub_graph_pb_kernel(tc, x_nodes, w1, b1, gamma, beta, w2, b2, out):
             kept["mean", unit] = mean
 
         def sum_squares(unit):
-            sq_sum = two.tile([P, TILES], F32)
+            sq_sum = every.tile([P, TILES], F32)
             for i in range(TILES):
                 squares = two.tile([P, H], BF16)
                 nc.scalar.activation(
@@ -236,7 +237,7 @@ def tile_sub_graph_pb_kernel(tc, x_nodes, w1, b1, gamma, beta, w2, b2, out):
             kept["sq_sum", unit] = sq_sum
 
         def take_root(unit):
-            inv_std = two.tile([P, TILES], F32)
+            inv_std = every.tile([P, TILES], F32)
             nc.scalar.activation(
                 out=inv_std[:],
                 in_=kept["sq_sum", unit][:],
@@ -247,7 +248,7 @@ def tile_sub_graph_pb_kernel(tc, x_nodes, w1, b1, gamma, beta, w2, b2, out):
             kept["inv_std", unit] = inv_std
 
         def scale_mean(unit):
-            shift = two.tile([P, TILES], F32)
+            shift = every.tile([P, TILES], F32)
             nc.vector.scalar_tensor_tensor(
                 out=shift[:],
                 in0=kept["mean", unit][:],
@@ -286,7 +287,7 @@ def tile_sub_graph_pb_kernel(tc, x_nodes, w1, b1, gamma, beta, w2, b2, out):
                 kept["zT", unit, bank] = zT
 
         def scale_relu(unit):
-            r_planes = three.tile([P, H_CHUNKS, UNIT], BF16)
+            r_planes = every.tile([P, H_CHUNKS, UNIT], BF16)
             for t in range(H_CHUNKS):
                 nc.scalar.activation(
                     out=r_planes[:, t, :],

@@ -304,8 +304,8 @@ def tile_sub_graph_pb_kernel(tc, x_nodes, w1, b1, gamma, beta, w2, b2, out):
                 group_words(nc.vector.tensor_copy, r_grouped, kept["r_planes", unit])
             else:
                 nc.gpsimd.tensor_scalar(
-                    out=r_grouped[:].rearrange("p (c i) t -> p c t i", i=RUN),
-                    in0=kept["r_planes", unit][:].rearrange("p t (c i) -> p c t i", i=RUN),
+                    out=r_grouped[:],
+                    in0=kept["r_planes", unit][:].rearrange("p t c -> p c t"),
                     scalar1=1.0,
                     scalar2=0.0,
                     op0=ALU.mult,

@@ -58,6 +58,7 @@ def tile_sub_graph_pb_kernel(tc, x_nodes, w1, b1, gamma, beta, w2, b2, out):
         const = ctx.enter_context(tc.tile_pool(name="const", bufs=1))
         x_pool = ctx.enter_context(tc.tile_pool(name="x", bufs=UNITS))
         two = ctx.enter_context(tc.tile_pool(name="two", bufs=2))
+        four = ctx.enter_context(tc.tile_pool(name="four", bufs=4))
         every = ctx.enter_context(tc.tile_pool(name="every", bufs=UNITS))
         one = ctx.enter_context(tc.tile_pool(name="one", bufs=1))
         three = ctx.enter_context(tc.tile_pool(name="three", bufs=3))
@@ -172,7 +173,7 @@ def tile_sub_graph_pb_kernel(tc, x_nodes, w1, b1, gamma, beta, w2, b2, out):
 
         def group_x(unit, tiles=range(TILES)):
             if tiles[0] == 0:
-                kept["x_grouped", unit] = two.tile([P, UNIT, PACK], BF16, name="x_grouped", align_bytes=64)
+                kept["x_grouped", unit] = four.tile([P, UNIT, PACK], BF16, name="x_grouped", align_bytes=64)
             nc.scalar.copy(
                 out=kept["x_grouped", unit][:]
                 .rearrange("p c t -> p (c t)")
@@ -183,8 +184,8 @@ def tile_sub_graph_pb_kernel(tc, x_nodes, w1, b1, gamma, beta, w2, b2, out):
 
         def quantise_x(unit, tiles=range(TILES)):
             if tiles[0] == 0:
-                kept["x_codes", unit] = three.tile([P, UNIT], U32, name="x_codes", align_bytes=64)
-                kept["x_scales", unit] = three.tile([P, UNIT], U8, name="x_scales", align_bytes=64)
+                kept["x_codes", unit] = four.tile([P, UNIT], U32, name="x_codes", align_bytes=64)
+                kept["x_scales", unit] = four.tile([P, UNIT], U8, name="x_scales", align_bytes=64)
             quantise(
                 nc,
                 kept["x_codes", unit][:, columns(tiles)],
@@ -225,7 +226,7 @@ def tile_sub_graph_pb_kernel(tc, x_nodes, w1, b1, gamma, beta, w2, b2, out):
         def sum_squares(unit):
             sq_sum = every.tile([P, TILES], F32)
             for i in range(TILES):
-                squares = two.tile([P, H], BF16)
+                squares = four.tile([P, H], BF16)
                 nc.scalar.activation(
                     out=squares[:],
                     in_=kept["h", unit][:, i, :],
@@ -261,7 +262,7 @@ def tile_sub_graph_pb_kernel(tc, x_nodes, w1, b1, gamma, beta, w2, b2, out):
 
         def normalise(engine, unit, i):
             if i == 0:
-                kept["z", unit] = two.tile([P, TILES, H], F32, name="z")
+                kept["z", unit] = four.tile([P, TILES, H], F32, name="z")
             z = kept["z", unit]
             engine.tensor_scalar(
                 out=z[:, i, :],
@@ -288,7 +289,7 @@ def tile_sub_graph_pb_kernel(tc, x_nodes, w1, b1, gamma, beta, w2, b2, out):
 
         def scale_relu(unit):
             r_planes = every.tile([P, H_CHUNKS, UNIT], BF16)
-            for t in range(H_CHUNKS):
+            for t in (1, 0, 3, 2):
                 nc.scalar.activation(
                     out=r_planes[:, t, :],
                     in_=kept["zT", unit, t // 2][:, t % 2, :],
@@ -314,8 +315,8 @@ def tile_sub_graph_pb_kernel(tc, x_nodes, w1, b1, gamma, beta, w2, b2, out):
             kept["r_grouped", unit] = r_grouped
 
         def quantise_r(unit):
-            r_codes = two.tile([P, UNIT], U32, align_bytes=64)
-            r_scales = two.tile([P, UNIT], U8, align_bytes=64)
+            r_codes = four.tile([P, UNIT], U32, align_bytes=64)
+            r_scales = four.tile([P, UNIT], U8, align_bytes=64)
             quantise(nc, r_codes[:], r_scales[:], kept["r_grouped", unit][:])
             kept["r_codes", unit] = r_codes
             kept["r_scales", unit] = r_scales
@@ -335,12 +336,13 @@ def tile_sub_graph_pb_kernel(tc, x_nodes, w1, b1, gamma, beta, w2, b2, out):
             kept["x1_ps", unit] = x1_ps
 
         def take_max(unit):
-            nc.vector.tensor_reduce(
-                out=best[:, :, unit * LINES_PER_UNIT : (unit + 1) * LINES_PER_UNIT],
-                in_=kept["x1_ps", unit][:].rearrange("m c (b l) -> m c b l", l=NODES),
-                axis=AXIS.X,
-                op=ALU.max,
-            )
+            for chunks in ([0], [1]) if unit == UNITS - 1 else ([0, 1],):
+                nc.vector.tensor_reduce(
+                    out=best[:, chunks[0] : chunks[-1] + 1, unit * LINES_PER_UNIT : (unit + 1) * LINES_PER_UNIT],
+                    in_=kept["x1_ps", unit][:, chunks[0] : chunks[-1] + 1, :].rearrange("m c (b l) -> m c b l", l=NODES),
+                    axis=AXIS.X,
+                    op=ALU.max,
+                )
 
         def at(step, unit):
             if 0 <= unit < UNITS:
@@ -378,9 +380,9 @@ def tile_sub_graph_pb_kernel(tc, x_nodes, w1, b1, gamma, beta, w2, b2, out):
             at(transpose_z, now - 4)
             at(scale_relu, now - 4)
             at(quantise_r, now - 5)
-            at(multiply_w2, now - 6)
             at(multiply_w1, now)
             at(transpose_x, now + 2)
+            at(multiply_w2, now - 6)
             if now == 1:
                 group_words(nc.vector.tensor_copy, w2_grouped, w2_raw)
             if now == 2:
@@ -389,10 +391,11 @@ def tile_sub_graph_pb_kernel(tc, x_nodes, w1, b1, gamma, beta, w2, b2, out):
             if now == 5:
                 spread_b2()
 
-        outT = psum_x.tile([P, G_CHUNKS, P], F32, name="outT", tag="xT")
+        out_sb = const.tile([P, G_CHUNKS, P], F32)
         for c in range(G_CHUNKS):
-            nc.tensor.transpose(out=outT[:, c, :], in_=best[:, c, :], identity=ident[:])
-        out_sb = const.tile([P, G], F32)
-        nc.vector.tensor_add(out=out_sb[:], in0=outT[:].rearrange("b c m -> b (c m)"), in1=b2_all[:])
-        nc.sync.dma_start(out=out[:, 0:G], in_=out_sb[0:POLYLINES, :])
-        nc.scalar.dma_start(out=out[:, G : 2 * G], in_=out_sb[0:POLYLINES, :])
+            outT = psum_h.tile([P, P], F32, tag="h_ps", name="outT")
+            nc.tensor.transpose(out=outT[:], in_=best[:, c, :], identity=ident[:])
+            nc.vector.tensor_add(out=out_sb[:, c, :], in0=outT[:], in1=b2_all[:, c * P : (c + 1) * P])
+            for half, queue in enumerate((nc.sync, nc.scalar)):
+                first = half * G + c * P
+                queue.dma_start(out=out[:, first : first + P], in_=out_sb[0:POLYLINES, c, :])

@@ -323,7 +323,7 @@ def tile_sub_graph_pb_kernel(tc, x_nodes, w1, b1, gamma, beta, w2, b2, out):
 
         def multiply_w2(unit):
             x1_ps = psum_x1.tile([P, G_CHUNKS, UNIT], F32, tag="x1_ps")
-            for c in range(G_CHUNKS):
+            for c in (0, 1, 0, 1):
                 nc.tensor.matmul_mx(
                     out=x1_ps[:, c, :],
                     lhsT=w2_codes[:, c * P : (c + 1) * P].bitcast(FP8X4),

@@ -28,6 +28,8 @@ G_CHUNKS = G // P
 LINES_PER_UNIT = UNIT // NODES
 WORDS = H // 2
 VECTOR_GROUPS = 4
+X_AHEAD = 1
+R_LAG = 5
 LAST_LAG = 7
 RUN = 4
 
@@ -36,7 +38,7 @@ FLOPS = 2 * TOKENS * H * H + 2 * TOKENS * H * G
 
 def group_words(copy, grouped, planes):
     copy(
-        out=grouped[:].rearrange("p (c i) t -> p c t i", i=RUN),
+        out=grouped.rearrange("p (c i) t -> p c t i", i=RUN),
         in_=planes[:].rearrange("p t (c i) -> p c t i", i=RUN),
     )
 
@@ -125,6 +127,8 @@ def tile_sub_graph_pb_kernel(tc, x_nodes, w1, b1, gamma, beta, w2, b2, out):
         w2_scales = const.tile([P, G], U8, align_bytes=64)
 
         kept = {}
+        shared_r = range(0, UNITS - R_LAG - X_AHEAD)
+        shared_x = range(R_LAG + X_AHEAD, UNITS)
 
         def group_w1():
             grouped = w1_grouped[:].rearrange("p (t m) j -> p t m j", t=PACK)
@@ -146,13 +150,23 @@ def tile_sub_graph_pb_kernel(tc, x_nodes, w1, b1, gamma, beta, w2, b2, out):
             )
 
         def widen_vectors():
-            nc.vector.tensor_copy(out=gamma_cols[:], in_=gamma_bf[:])
-            nc.vector.tensor_copy(out=beta_cols[:], in_=beta_bf[:])
+            nc.gpsimd.tensor_copy(out=gamma_cols[:], in_=gamma_bf[:])
+            nc.gpsimd.tensor_copy(out=beta_cols[:], in_=beta_bf[:])
 
         def spread_b2():
             b2_ps = psum_z.tile([P, G], F32, tag="zT")
             nc.tensor.matmul(out=b2_ps[:], lhsT=ones[:], rhs=b2_row[:], start=True, stop=True)
-            nc.vector.tensor_copy(out=b2_all[:], in_=b2_ps[:])
+            nc.scalar.copy(out=b2_all[:], in_=b2_ps[:])
+
+        def gpsimd_group(grouped, planes):
+            nc.gpsimd.tensor_scalar(
+                out=grouped,
+                in0=planes[:].rearrange("p t c -> p c t"),
+                scalar1=1.0,
+                scalar2=0.0,
+                op0=ALU.mult,
+                op1=ALU.add,
+            )
 
 
         def transpose_x(unit, tiles=range(TILES), pool=psum_x, tag="xT"):
@@ -172,10 +186,14 @@ def tile_sub_graph_pb_kernel(tc, x_nodes, w1, b1, gamma, beta, w2, b2, out):
             return slice(tiles[0] * P, (tiles[-1] + 1) * P)
 
         def group_x(unit, tiles=range(TILES)):
-            if tiles[0] == 0:
-                kept["x_grouped", unit] = four.tile([P, UNIT, PACK], BF16, name="x_grouped", align_bytes=64)
+            if unit in shared_x:
+                kept["mixed", unit] = one.tile([P, 2 * UNIT, PACK], BF16, name="mixed", align_bytes=64)
+                kept["x_grouped", unit] = kept["mixed", unit][:, 0:UNIT, :]
+            elif tiles[0] == 0:
+                x_grouped = four.tile([P, UNIT, PACK], BF16, align_bytes=64)
+                kept["x_grouped", unit] = x_grouped[:]
             nc.scalar.copy(
-                out=kept["x_grouped", unit][:]
+                out=kept["x_grouped", unit]
                 .rearrange("p c t -> p (c t)")
                 .bitcast(F32)
                 .rearrange("p (i c u) -> p i c u", i=TILES, u=2)[:, tiles[0] : tiles[-1] + 1, :, :],
@@ -184,8 +202,10 @@ def tile_sub_graph_pb_kernel(tc, x_nodes, w1, b1, gamma, beta, w2, b2, out):
 
         def quantise_x(unit, tiles=range(TILES)):
             if tiles[0] == 0:
-                kept["x_codes", unit] = four.tile([P, UNIT], U32, name="x_codes", align_bytes=64)
-                kept["x_scales", unit] = four.tile([P, UNIT], U8, name="x_scales", align_bytes=64)
+                x_codes = four.tile([P, UNIT], U32, align_bytes=64)
+                x_scales = four.tile([P, UNIT], U8, align_bytes=64)
+                kept["x_codes", unit] = x_codes[:]
+                kept["x_scales", unit] = x_scales[:]
             quantise(
                 nc,
                 kept["x_codes", unit][:, columns(tiles)],
@@ -249,16 +269,9 @@ def tile_sub_graph_pb_kernel(tc, x_nodes, w1, b1, gamma, beta, w2, b2, out):
             kept["inv_std", unit] = inv_std
 
         def scale_mean(unit):
-            shift = every.tile([P, TILES], F32)
-            nc.vector.scalar_tensor_tensor(
-                out=shift[:],
-                in0=kept["mean", unit][:],
-                scalar=-1.0 / H,
-                in1=kept["inv_std", unit][:],
-                op0=ALU.mult,
-                op1=ALU.mult,
-            )
-            kept["shift", unit] = shift
+            small_mean = every.tile([P, TILES], F32)
+            nc.scalar.mul(out=small_mean[:], in_=kept["mean", unit][:], mul=1.0 / H)
+            kept["small_mean", unit] = small_mean
 
         def normalise(engine, unit, i):
             if i == 0:
@@ -267,10 +280,10 @@ def tile_sub_graph_pb_kernel(tc, x_nodes, w1, b1, gamma, beta, w2, b2, out):
             engine.tensor_scalar(
                 out=z[:, i, :],
                 in0=kept["h", unit][:, i, :],
-                scalar1=kept["inv_std", unit][:, i : i + 1],
-                scalar2=kept["shift", unit][:, i : i + 1],
-                op0=ALU.mult,
-                op1=ALU.add,
+                scalar1=kept["small_mean", unit][:, i : i + 1],
+                scalar2=kept["inv_std", unit][:, i : i + 1],
+                op0=ALU.subtract,
+                op1=ALU.mult,
             )
 
 
@@ -300,26 +313,33 @@ def tile_sub_graph_pb_kernel(tc, x_nodes, w1, b1, gamma, beta, w2, b2, out):
             kept["r_planes", unit] = r_planes
 
         def group_r(unit):
-            r_grouped = one.tile([P, UNIT, PACK], BF16, align_bytes=64)
+            if unit in shared_r:
+                r_grouped = kept["mixed", unit + R_LAG + X_AHEAD][:, UNIT : 2 * UNIT, :]
+            else:
+                r_alone = two.tile([P, UNIT, PACK], BF16, align_bytes=64)
+                r_grouped = r_alone[:]
             if unit >= UNITS - VECTOR_GROUPS:
                 group_words(nc.vector.tensor_copy, r_grouped, kept["r_planes", unit])
             else:
-                nc.gpsimd.tensor_scalar(
-                    out=r_grouped[:],
-                    in0=kept["r_planes", unit][:].rearrange("p t c -> p c t"),
-                    scalar1=1.0,
-                    scalar2=0.0,
-                    op0=ALU.mult,
-                    op1=ALU.add,
-                )
+                gpsimd_group(r_grouped, kept["r_planes", unit])
             kept["r_grouped", unit] = r_grouped
 
         def quantise_r(unit):
             r_codes = four.tile([P, UNIT], U32, align_bytes=64)
             r_scales = four.tile([P, UNIT], U8, align_bytes=64)
-            quantise(nc, r_codes[:], r_scales[:], kept["r_grouped", unit][:])
-            kept["r_codes", unit] = r_codes
-            kept["r_scales", unit] = r_scales
+            quantise(nc, r_codes[:], r_scales[:], kept["r_grouped", unit])
+            kept["r_codes", unit] = r_codes[:]
+            kept["r_scales", unit] = r_scales[:]
+
+        def quantise_both(unit):
+            x_unit = unit + R_LAG + X_AHEAD
+            codes = four.tile([P, 2 * UNIT], U32, align_bytes=64)
+            scales = four.tile([P, 2 * UNIT], U8, align_bytes=64)
+            quantise(nc, codes[:], scales[:], kept["mixed", x_unit][:])
+            kept["x_codes", x_unit] = codes[:, 0:UNIT]
+            kept["x_scales", x_unit] = scales[:, 0:UNIT]
+            kept["r_codes", unit] = codes[:, UNIT : 2 * UNIT]
+            kept["r_scales", unit] = scales[:, UNIT : 2 * UNIT]
 
         def multiply_w2(unit):
             x1_ps = psum_x1.tile([P, G_CHUNKS, UNIT], F32, tag="x1_ps")
@@ -328,8 +348,8 @@ def tile_sub_graph_pb_kernel(tc, x_nodes, w1, b1, gamma, beta, w2, b2, out):
                     out=x1_ps[:, c, :],
                     lhsT=w2_codes[:, c * P : (c + 1) * P].bitcast(FP8X4),
                     lhsT_scale=w2_scales[:, c * P : (c + 1) * P],
-                    rhs=kept["r_codes", unit][:].bitcast(FP8X4),
-                    rhs_scale=kept["r_scales", unit][:],
+                    rhs=kept["r_codes", unit].bitcast(FP8X4),
+                    rhs_scale=kept["r_scales", unit],
                     start=True,
                     stop=True,
                 )
@@ -366,27 +386,31 @@ def tile_sub_graph_pb_kernel(tc, x_nodes, w1, b1, gamma, beta, w2, b2, out):
         for now in range(1, UNITS + LAST_LAG):
             at(sum_squares, now - 2)
             at(group_x, now + 1)
+            at(scale_mean, now - 2)
             at(take_root, now - 2)
             if now < UNITS + 1:
                 at(group_r, now - 5)
             at(add_b1, now - 1)
             at(take_max, now - 7)
-            at(scale_mean, now - 3)
-            at(quantise_x, now + 1)
+            if now + X_AHEAD not in shared_x:
+                at(quantise_x, now + X_AHEAD)
             if now >= UNITS + 1:
                 at(group_r, now - 5)
             at(lambda unit: normalise(nc.vector, unit, 0), now - 3)
             at(lambda unit: normalise(nc.vector, unit, 1), now - 3)
             at(transpose_z, now - 4)
             at(scale_relu, now - 4)
-            at(quantise_r, now - 5)
+            if now - R_LAG in shared_r:
+                quantise_both(now - R_LAG)
+            else:
+                at(quantise_r, now - R_LAG)
             at(multiply_w1, now)
             at(transpose_x, now + 2)
             at(multiply_w2, now - 6)
             if now == 1:
-                group_words(nc.vector.tensor_copy, w2_grouped, w2_raw)
-            if now == 2:
+                gpsimd_group(w2_grouped[:], w2_raw)
                 widen_vectors()
+            if now == 2:
                 quantise(nc, w2_codes[:], w2_scales[:], w2_grouped[:])
             if now == 5:
                 spread_b2()

@@ -30,6 +30,7 @@ WORDS = H // 2
 VECTOR_GROUPS = 4
 X_AHEAD = 1
 R_LAG = 5
+H_BANKS = 4
 LAST_LAG = 7
 RUN = 4
 
@@ -65,7 +66,7 @@ def tile_sub_graph_pb_kernel(tc, x_nodes, w1, b1, gamma, beta, w2, b2, out):
         one = ctx.enter_context(tc.tile_pool(name="one", bufs=1))
         three = ctx.enter_context(tc.tile_pool(name="three", bufs=3))
         psum_x = ctx.enter_context(tc.psum_pool(name="psum_x", bufs=1))
-        psum_h = ctx.enter_context(tc.psum_pool(name="psum_h", bufs=2 * TILES))
+        psum_h = ctx.enter_context(tc.psum_pool(name="psum_h", bufs=H_BANKS))
         psum_z = ctx.enter_context(tc.psum_pool(name="psum_z", bufs=2))
         psum_x1 = ctx.enter_context(tc.psum_pool(name="psum_x1", bufs=1))
 
@@ -97,15 +98,17 @@ def tile_sub_graph_pb_kernel(tc, x_nodes, w1, b1, gamma, beta, w2, b2, out):
         load_x(0, [1])
         nc.sync.dma_start(out=b1_row[0:1, :], in_=b1.rearrange("(o c) -> o c", o=1))
         load_x(1)
+        load_x(2)
+        load_x(3)
         gamma_bf = const.tile([P, PACK], BF16)
         nc.sync.dma_start(out=gamma_bf[:], in_=gamma.rearrange("(p t) -> p t", t=PACK))
         beta_bf = const.tile([P, PACK], BF16)
         nc.sync.dma_start(out=beta_bf[:], in_=beta.rearrange("(p t) -> p t", t=PACK))
-        load_x(2)
+        load_x(4)
         w2_raw = const.tile([P, PACK, G], BF16)
         nc.sync.dma_start(out=w2_raw[:], in_=w2.rearrange("(p j) c -> p j c", j=PACK))
         nc.sync.dma_start(out=b2_row[0:1, :], in_=b2.rearrange("(o c) -> o c", o=1))
-        for unit in range(3, UNITS):
+        for unit in range(5, UNITS):
             load_x(unit)
 
         ident = const.tile([P, P], F32)
@@ -342,7 +345,8 @@ def tile_sub_graph_pb_kernel(tc, x_nodes, w1, b1, gamma, beta, w2, b2, out):
             kept["r_scales", unit] = scales[:, UNIT : 2 * UNIT]
 
         def multiply_w2(unit):
-            x1_ps = psum_x1.tile([P, G_CHUNKS, UNIT], F32, tag="x1_ps")
+            pool, tag = (psum_h, "h_ps") if unit >= UNITS - H_BANKS else (psum_x1, "x1_ps")
+            x1_ps = pool.tile([P, G_CHUNKS, UNIT], F32, tag=tag, name="x1_ps")
             for c in (0, 1, 0, 1):
                 nc.tensor.matmul_mx(
                     out=x1_ps[:, c, :],
@@ -407,10 +411,11 @@ def tile_sub_graph_pb_kernel(tc, x_nodes, w1, b1, gamma, beta, w2, b2, out):
             at(multiply_w1, now)
             at(transpose_x, now + 2)
             at(multiply_w2, now - 6)
-            if now == 1:
-                gpsimd_group(w2_grouped[:], w2_raw)
+            if now == 3:
                 widen_vectors()
-            if now == 2:
+            if now == 4:
+                group_words(nc.vector.tensor_copy, w2_grouped[:], w2_raw)
+            if now == 5:
                 quantise(nc, w2_codes[:], w2_scales[:], w2_grouped[:])
             if now == 5:
                 spread_b2()

@@ -30,6 +30,9 @@ WORDS = H // 2
 VECTOR_GROUPS = 4
 X_AHEAD = 1
 R_LAG = 5
+X_PLACE = (0, 2 * UNIT)
+R_PLACE = UNIT
+X_BANK_X1 = range(UNITS - 5, UNITS, 2)
 H_BANKS = 4
 LAST_LAG = 7
 RUN = 4
@@ -63,8 +66,6 @@ def tile_sub_graph_pb_kernel(tc, x_nodes, w1, b1, gamma, beta, w2, b2, out):
         two = ctx.enter_context(tc.tile_pool(name="two", bufs=2))
         four = ctx.enter_context(tc.tile_pool(name="four", bufs=4))
         every = ctx.enter_context(tc.tile_pool(name="every", bufs=UNITS))
-        one = ctx.enter_context(tc.tile_pool(name="one", bufs=1))
-        three = ctx.enter_context(tc.tile_pool(name="three", bufs=3))
         psum_x = ctx.enter_context(tc.psum_pool(name="psum_x", bufs=1))
         psum_h = ctx.enter_context(tc.psum_pool(name="psum_h", bufs=H_BANKS))
         psum_z = ctx.enter_context(tc.psum_pool(name="psum_z", bufs=2))
@@ -129,6 +130,7 @@ def tile_sub_graph_pb_kernel(tc, x_nodes, w1, b1, gamma, beta, w2, b2, out):
         w2_codes = const.tile([P, G], U32, align_bytes=64)
         w2_scales = const.tile([P, G], U8, align_bytes=64)
 
+        mixed = const.tile([P, 3 * UNIT, PACK], BF16, align_bytes=64)
         kept = {}
         shared_r = range(0, UNITS - R_LAG - X_AHEAD)
         shared_x = range(R_LAG + X_AHEAD, UNITS)
@@ -190,8 +192,7 @@ def tile_sub_graph_pb_kernel(tc, x_nodes, w1, b1, gamma, beta, w2, b2, out):
 
         def group_x(unit, tiles=range(TILES)):
             if unit in shared_x:
-                kept["mixed", unit] = one.tile([P, 2 * UNIT, PACK], BF16, name="mixed", align_bytes=64)
-                kept["x_grouped", unit] = kept["mixed", unit][:, 0:UNIT, :]
+                kept["x_grouped", unit] = mixed[:, X_PLACE[unit % 2] : X_PLACE[unit % 2] + UNIT, :]
             elif tiles[0] == 0:
                 x_grouped = four.tile([P, UNIT, PACK], BF16, align_bytes=64)
                 kept["x_grouped", unit] = x_grouped[:]
@@ -276,23 +277,23 @@ def tile_sub_graph_pb_kernel(tc, x_nodes, w1, b1, gamma, beta, w2, b2, out):
             nc.scalar.mul(out=small_mean[:], in_=kept["mean", unit][:], mul=1.0 / H)
             kept["small_mean", unit] = small_mean
 
-        def normalise(engine, unit, i):
-            if i == 0:
-                kept["z", unit] = four.tile([P, TILES, H], F32, name="z")
-            z = kept["z", unit]
-            engine.tensor_scalar(
-                out=z[:, i, :],
-                in0=kept["h", unit][:, i, :],
-                scalar1=kept["small_mean", unit][:, i : i + 1],
-                scalar2=kept["inv_std", unit][:, i : i + 1],
-                op0=ALU.subtract,
-                op1=ALU.mult,
-            )
-
+        def normalise(unit):
+            z = four.tile([P, TILES, H], F32)
+            for i in range(TILES):
+                nc.vector.tensor_scalar(
+                    out=z[:, i, :],
+                    in0=kept["h", unit][:, i, :],
+                    scalar1=kept["small_mean", unit][:, i : i + 1],
+                    scalar2=kept["inv_std", unit][:, i : i + 1],
+                    op0=ALU.subtract,
+                    op1=ALU.mult,
+                )
+            kept["z", unit] = z
 
         def transpose_z(unit):
             for bank in range(2):
-                zT = psum_z.tile([P, 2, UNIT], F32, tag="zT")
+                pool, tag = (psum_h, "h_ps") if unit >= UNITS - 2 else (psum_z, "zT")
+                zT = pool.tile([P, 2, UNIT], F32, tag=tag, name="zT")
                 for s in range(2):
                     t = 2 * bank + s
                     for i in range(TILES):
@@ -317,7 +318,7 @@ def tile_sub_graph_pb_kernel(tc, x_nodes, w1, b1, gamma, beta, w2, b2, out):
 
         def group_r(unit):
             if unit in shared_r:
-                r_grouped = kept["mixed", unit + R_LAG + X_AHEAD][:, UNIT : 2 * UNIT, :]
+                r_grouped = mixed[:, R_PLACE : R_PLACE + UNIT, :]
             else:
                 r_alone = two.tile([P, UNIT, PACK], BF16, align_bytes=64)
                 r_grouped = r_alone[:]
@@ -338,14 +339,17 @@ def tile_sub_graph_pb_kernel(tc, x_nodes, w1, b1, gamma, beta, w2, b2, out):
             x_unit = unit + R_LAG + X_AHEAD
             codes = four.tile([P, 2 * UNIT], U32, align_bytes=64)
             scales = four.tile([P, 2 * UNIT], U8, align_bytes=64)
-            quantise(nc, codes[:], scales[:], kept["mixed", x_unit][:])
-            kept["x_codes", x_unit] = codes[:, 0:UNIT]
-            kept["x_scales", x_unit] = scales[:, 0:UNIT]
-            kept["r_codes", unit] = codes[:, UNIT : 2 * UNIT]
-            kept["r_scales", unit] = scales[:, UNIT : 2 * UNIT]
+            first = min(R_PLACE, X_PLACE[x_unit % 2])
+            quantise(nc, codes[:], scales[:], mixed[:, first : first + 2 * UNIT, :])
+            x_part = slice(X_PLACE[x_unit % 2] - first, X_PLACE[x_unit % 2] - first + UNIT)
+            r_part = slice(R_PLACE - first, R_PLACE - first + UNIT)
+            kept["x_codes", x_unit] = codes[:, x_part]
+            kept["x_scales", x_unit] = scales[:, x_part]
+            kept["r_codes", unit] = codes[:, r_part]
+            kept["r_scales", unit] = scales[:, r_part]
 
         def multiply_w2(unit):
-            pool, tag = (psum_h, "h_ps") if unit >= UNITS - H_BANKS else (psum_x1, "x1_ps")
+            pool, tag = (psum_x, "xT") if unit in X_BANK_X1 else (psum_x1, "x1_ps")
             x1_ps = pool.tile([P, G_CHUNKS, UNIT], F32, tag=tag, name="x1_ps")
             for c in (0, 1, 0, 1):
                 nc.tensor.matmul_mx(
@@ -381,6 +385,8 @@ def tile_sub_graph_pb_kernel(tc, x_nodes, w1, b1, gamma, beta, w2, b2, out):
         group_x(0, [1])
         group_x(1)
         transpose_x(2)
+        group_x(2)
+        transpose_x(3, pool=psum_z, tag="zT")
         quantise_x(0, [0])
         quantise(nc, w1_codes[:], w1_scales[:], w1_grouped[:])
         quantise_x(0, [1])
@@ -389,19 +395,21 @@ def tile_sub_graph_pb_kernel(tc, x_nodes, w1, b1, gamma, beta, w2, b2, out):
         multiply_w1(0)
         for now in range(1, UNITS + LAST_LAG):
             at(sum_squares, now - 2)
-            at(group_x, now + 1)
+            at(group_x, now + X_AHEAD + 1)
             at(scale_mean, now - 2)
             at(take_root, now - 2)
             if now < UNITS + 1:
                 at(group_r, now - 5)
             at(add_b1, now - 1)
-            at(take_max, now - 7)
-            if now + X_AHEAD not in shared_x:
-                at(quantise_x, now + X_AHEAD)
-            if now >= UNITS + 1:
+            if now < UNITS + 1:
+                at(take_max, now - 7)
+                if now + X_AHEAD not in shared_x:
+                    at(quantise_x, now + X_AHEAD)
+                at(normalise, now - 3)
+            else:
+                at(normalise, now - 3)
                 at(group_r, now - 5)
-            at(lambda unit: normalise(nc.vector, unit, 0), now - 3)
-            at(lambda unit: normalise(nc.vector, unit, 1), now - 3)
+                at(take_max, now - 7)
             at(transpose_z, now - 4)
             at(scale_relu, now - 4)
             if now - R_LAG in shared_r:
@@ -409,7 +417,7 @@ def tile_sub_graph_pb_kernel(tc, x_nodes, w1, b1, gamma, beta, w2, b2, out):
             else:
                 at(quantise_r, now - R_LAG)
             at(multiply_w1, now)
-            at(transpose_x, now + 2)
+            at(transpose_x, now + X_AHEAD + 2)
             at(multiply_w2, now - 6)
             if now == 3:
                 widen_vectors()
@@ -417,7 +425,7 @@ def tile_sub_graph_pb_kernel(tc, x_nodes, w1, b1, gamma, beta, w2, b2, out):
                 group_words(nc.vector.tensor_copy, w2_grouped[:], w2_raw)
             if now == 5:
                 quantise(nc, w2_codes[:], w2_scales[:], w2_grouped[:])
-            if now == 5:
+            if now == UNITS + 3:
                 spread_b2()
 
         out_sb = const.tile([P, G_CHUNKS, P], F32)

@@ -43,7 +43,7 @@ FLOPS = 2 * TOKENS * H * H + 2 * TOKENS * H * G
 def group_words(copy, grouped, planes):
     copy(
         out=grouped.rearrange("p (c i) t -> p c t i", i=RUN),
-        in_=planes[:].rearrange("p t (c i) -> p c t i", i=RUN),
+        in_=planes.rearrange("p t (c i) -> p c t i", i=RUN),
     )
 
 
@@ -166,7 +166,7 @@ def tile_sub_graph_pb_kernel(tc, x_nodes, w1, b1, gamma, beta, w2, b2, out):
         def gpsimd_group(grouped, planes):
             nc.gpsimd.tensor_scalar(
                 out=grouped,
-                in0=planes[:].rearrange("p t c -> p c t"),
+                in0=planes.rearrange("p t c -> p c t"),
                 scalar1=1.0,
                 scalar2=0.0,
                 op0=ALU.mult,
@@ -314,7 +314,7 @@ def tile_sub_graph_pb_kernel(tc, x_nodes, w1, b1, gamma, beta, w2, b2, out):
                     bias=beta_cols[:, t : t + 1],
                     scale=gamma_cols[:, t : t + 1],
                 )
-            kept["r_planes", unit] = r_planes
+            kept["r_planes", unit] = r_planes[:]
 
         def group_r(unit):
             if unit in shared_r:
@@ -322,7 +322,10 @@ def tile_sub_graph_pb_kernel(tc, x_nodes, w1, b1, gamma, beta, w2, b2, out):
             else:
                 r_alone = two.tile([P, UNIT, PACK], BF16, align_bytes=64)
                 r_grouped = r_alone[:]
-            if unit >= UNITS - VECTOR_GROUPS:
+            if unit == UNITS - 1:
+                for copy, part in ((nc.scalar.copy, columns([0])), (nc.vector.tensor_copy, columns([1]))):
+                    group_words(copy, r_grouped[:, part, :], kept["r_planes", unit][:, :, part])
+            elif unit >= UNITS - VECTOR_GROUPS:
                 group_words(nc.vector.tensor_copy, r_grouped, kept["r_planes", unit])
             else:
                 gpsimd_group(r_grouped, kept["r_planes", unit])
@@ -351,9 +354,13 @@ def tile_sub_graph_pb_kernel(tc, x_nodes, w1, b1, gamma, beta, w2, b2, out):
         def multiply_w2(unit):
             pool, tag = (psum_x, "xT") if unit in X_BANK_X1 else (psum_x1, "x1_ps")
             x1_ps = pool.tile([P, G_CHUNKS, UNIT], F32, tag=tag, name="x1_ps")
-            for c in (0, 1, 0, 1):
+            x1 = [x1_ps[:, c, :] for c in range(G_CHUNKS)]
+            if unit == UNITS - 1:
+                x1_late = psum_z.tile([P, UNIT], F32, tag="zT", name="x1_late")
+                x1[1] = x1_late[:]
+            for c in range(G_CHUNKS) if unit == UNITS - 1 else (0, 1, 0, 1):
                 nc.tensor.matmul_mx(
-                    out=x1_ps[:, c, :],
+                    out=x1[c],
                     lhsT=w2_codes[:, c * P : (c + 1) * P].bitcast(FP8X4),
                     lhsT_scale=w2_scales[:, c * P : (c + 1) * P],
                     rhs=kept["r_codes", unit].bitcast(FP8X4),
@@ -362,12 +369,22 @@ def tile_sub_graph_pb_kernel(tc, x_nodes, w1, b1, gamma, beta, w2, b2, out):
                     stop=True,
                 )
             kept["x1_ps", unit] = x1_ps
+            kept["x1", unit] = x1
 
         def take_max(unit):
-            for chunks in ([0], [1]) if unit == UNITS - 1 else ([0, 1],):
+            lines = slice(unit * LINES_PER_UNIT, (unit + 1) * LINES_PER_UNIT)
+            if unit == UNITS - 1:
+                for c in range(G_CHUNKS):
+                    nc.vector.tensor_reduce(
+                        out=best[:, c, lines],
+                        in_=kept["x1", unit][c].rearrange("m (b l) -> m b l", l=NODES),
+                        axis=AXIS.X,
+                        op=ALU.max,
+                    )
+            else:
                 nc.vector.tensor_reduce(
-                    out=best[:, chunks[0] : chunks[-1] + 1, unit * LINES_PER_UNIT : (unit + 1) * LINES_PER_UNIT],
-                    in_=kept["x1_ps", unit][:, chunks[0] : chunks[-1] + 1, :].rearrange("m c (b l) -> m c b l", l=NODES),
+                    out=best[:, :, lines],
+                    in_=kept["x1_ps", unit][:].rearrange("m c (b l) -> m c b l", l=NODES),
                     axis=AXIS.X,
                     op=ALU.max,
                 )
@@ -422,7 +439,7 @@ def tile_sub_graph_pb_kernel(tc, x_nodes, w1, b1, gamma, beta, w2, b2, out):
             if now == 3:
                 widen_vectors()
             if now == 4:
-                group_words(nc.vector.tensor_copy, w2_grouped[:], w2_raw)
+                group_words(nc.vector.tensor_copy, w2_grouped[:], w2_raw[:])
             if now == 5:
                 quantise(nc, w2_codes[:], w2_scales[:], w2_grouped[:])
             if now == UNITS + 3:

@@ -84,6 +84,10 @@ def tile_sub_graph_pb_kernel(tc, x_nodes, w1, b1, gamma, beta, w2, b2, out):
                 ),
             )
 
+        ones = const.tile([P, P], BF16)
+        nc.vector.memset(ones[:], 1.0)
+        blank = const.tile([P, H], BF16)
+        nc.vector.memset(blank[:], 0.0)
         eps_col = const.tile([P, 1], F32)
         nc.vector.memset(eps_col[:], EPS / H**2)
         warm = const.tile([P, 1], F32)
@@ -114,8 +118,6 @@ def tile_sub_graph_pb_kernel(tc, x_nodes, w1, b1, gamma, beta, w2, b2, out):
 
         ident = const.tile([P, P], F32)
         masks.make_identity(nc, ident[:])
-        ones = const.tile([P, P], BF16)
-        nc.vector.memset(ones[:], 1.0)
         best = const.tile([P, G_CHUNKS, P], F32)
         nc.vector.memset(best[:], 0.0)
         b1_all = const.tile([P, H], F32)
@@ -153,6 +155,11 @@ def tile_sub_graph_pb_kernel(tc, x_nodes, w1, b1, gamma, beta, w2, b2, out):
                 in0=kept["b1_ps"][:].rearrange("p (m t) -> p t m", t=PACK),
                 scalar1=1.0 / H,
             )
+
+        def warm_up():
+            waste = psum_x1.tile([P, H], F32, tag="x1_ps", name="waste")
+            for turn in range(4):
+                nc.tensor.matmul(out=waste[:], lhsT=ones[:], rhs=blank[:], start=True, stop=True)
 
         def widen_vectors():
             nc.gpsimd.tensor_copy(out=gamma_cols[:], in_=gamma_bf[:])
@@ -393,6 +400,7 @@ def tile_sub_graph_pb_kernel(tc, x_nodes, w1, b1, gamma, beta, w2, b2, out):
             if 0 <= unit < UNITS:
                 step(unit)
 
+        warm_up()
         for i in range(TILES):
             transpose_x(0, [i])
         spread_b1()

from contextlib import ExitStack

import concourse.masks as masks
import concourse.mybir as mybir

F32 = mybir.dt.float32
BF16 = mybir.dt.bfloat16
U32 = mybir.dt.uint32
U8 = mybir.dt.uint8
FP8X4 = mybir.dt.float8_e4m3fn_x4
ALU = mybir.AluOpType
ACT = mybir.ActivationFunctionType
AXIS = mybir.AxisListType

P = 128
PACK = 4
POLYLINES = 64
NODES = 64
H = 512
G = 256
EPS = 1e-5
TOKENS = POLYLINES * NODES
TILES = 2
UNIT = TILES * P
UNITS = TOKENS // UNIT
H_CHUNKS = H // P
G_CHUNKS = G // P
LINES_PER_UNIT = UNIT // NODES
WORDS = H // 2
VECTOR_GROUPS = 4
X_AHEAD = 1
R_LAG = 5
X_PLACE = (0, 2 * UNIT)
R_PLACE = UNIT
X_BANK_X1 = range(UNITS - 5, UNITS, 2)
H_BANKS = 4
LAST_LAG = 7
RUN = 4

FLOPS = 2 * TOKENS * H * H + 2 * TOKENS * H * G


def group_words(copy, grouped, planes):
    copy(
        out=grouped.rearrange("p (c i) t -> p c t i", i=RUN),
        in_=planes.rearrange("p t (c i) -> p c t i", i=RUN),
    )


def quantise(nc, codes, scales, grouped):
    nc.vector.quantize_mx(
        out=codes.bitcast(FP8X4),
        scales=scales,
        in_=grouped.rearrange("p c t -> p (c t)"),
    )


def tile_sub_graph_pb_kernel(tc, x_nodes, w1, b1, gamma, beta, w2, b2, out):
    nc = tc.nc
    x_flat = x_nodes.rearrange("b l k -> (b l) k")

    with ExitStack() as ctx:
        ctx.enter_context(tc.manual_schedule())
        const = ctx.enter_context(tc.tile_pool(name="const", bufs=1))
        x_pool = ctx.enter_context(tc.tile_pool(name="x", bufs=UNITS))
        two = ctx.enter_context(tc.tile_pool(name="two", bufs=2))
        four = ctx.enter_context(tc.tile_pool(name="four", bufs=4))
        every = ctx.enter_context(tc.tile_pool(name="every", bufs=UNITS))
        psum_x = ctx.enter_context(tc.psum_pool(name="psum_x", bufs=1))
        psum_h = ctx.enter_context(tc.psum_pool(name="psum_h", bufs=H_BANKS))
        psum_z = ctx.enter_context(tc.psum_pool(name="psum_z", bufs=2))
        psum_x1 = ctx.enter_context(tc.psum_pool(name="psum_x1", bufs=1))

        x_sb = {}

        def load_x(unit, tiles=range(TILES)):
            if unit not in x_sb:
                x_sb[unit] = x_pool.tile([P, TILES * H], BF16, name="x_sb")
            first, count = tiles[0], len(tiles)
            nc.sync.dma_start(
                out=x_sb[unit][:, first * H : (first + count) * H].rearrange("p (i k) -> p i k", i=count),
                in_=x_flat[unit * UNIT + first * P : unit * UNIT + (first + count) * P, :].rearrange(
                    "(i p) k -> p i k", p=P
                ),
            )

        ones = const.tile([P, P], BF16)
        nc.vector.memset(ones[:], 1.0)
        blank = const.tile([P, H], BF16)
        nc.vector.memset(blank[:], 0.0)
        eps_col = const.tile([P, 1], F32)
        nc.vector.memset(eps_col[:], EPS / H**2)
        warm = const.tile([P, 1], F32)
        nc.scalar.activation(out=warm[:], in_=eps_col[:], func=ACT.Abs_reciprocal_sqrt)
        b1_row = const.tile([P, H], BF16)
        nc.vector.memset(b1_row[:], 0.0)
        b2_row = const.tile([P, G], BF16)
        nc.vector.memset(b2_row[:], 0.0)

        w1_raw = const.tile([P, PACK, H], BF16)
        load_x(0, [0])
        nc.sync.dma_start(out=w1_raw[:], in_=w1.rearrange("(p j) c -> p j c", j=PACK))
        load_x(0, [1])
        nc.sync.dma_start(out=b1_row[0:1, :], in_=b1.rearrange("(o c) -> o c", o=1))
        load_x(1)
        load_x(2)
        load_x(3)
        gamma_bf = const.tile([P, PACK], BF16)
        nc.sync.dma_start(out=gamma_bf[:], in_=gamma.rearrange("(p t) -> p t", t=PACK))
        beta_bf = const.tile([P, PACK], BF16)
        nc.sync.dma_start(out=beta_bf[:], in_=beta.rearrange("(p t) -> p t", t=PACK))
        load_x(4)
        w2_raw = const.tile([P, PACK, G], BF16)
        nc.sync.dma_start(out=w2_raw[:], in_=w2.rearrange("(p j) c -> p j c", j=PACK))
        nc.sync.dma_start(out=b2_row[0:1, :], in_=b2.rearrange("(o c) -> o c", o=1))
        for unit in range(5, UNITS):
            load_x(unit)

        ident = const.tile([P, P], F32)
        masks.make_identity(nc, ident[:])
        best = const.tile([P, G_CHUNKS, P], F32)
        nc.vector.memset(best[:], 0.0)
        b1_all = const.tile([P, H], F32)
        gamma_cols = const.tile([P, PACK], F32)
        beta_cols = const.tile([P, PACK], F32)
        b2_all = const.tile([P, G], F32)

        w1_grouped = const.tile([P, H, PACK], BF16, align_bytes=64)
        w1_codes = const.tile([P, H], U32, align_bytes=64)
        w1_scales = const.tile([P, H], U8, align_bytes=64)
        w2_grouped = const.tile([P, G, PACK], BF16, align_bytes=64)
        w2_codes = const.tile([P, G], U32, align_bytes=64)
        w2_scales = const.tile([P, G], U8, align_bytes=64)

        mixed = const.tile([P, 3 * UNIT, PACK], BF16, align_bytes=64)
        kept = {}
        shared_r = range(0, UNITS - R_LAG - X_AHEAD)
        shared_x = range(R_LAG + X_AHEAD, UNITS)

        def group_w1():
            grouped = w1_grouped[:].rearrange("p (t m) j -> p t m j", t=PACK)
            raw = w1_raw[:].rearrange("p j (m t) -> p t m j", t=PACK)
            nc.scalar.copy(out=grouped[:, 3, :, :], in_=raw[:, 3, :, :])
            nc.vector.tensor_copy(out=grouped[:, 0:2, :, :], in_=raw[:, 0:2, :, :])
            nc.vector.tensor_copy(out=grouped[:, 2, :, :], in_=raw[:, 2, :, :])

        def spread_b1():
            b1_ps = psum_z.tile([P, H], F32, tag="zT")
            kept["b1_ps"] = b1_ps
            nc.tensor.matmul(out=b1_ps[:], lhsT=ones[:], rhs=b1_row[:], start=True, stop=True)

        def place_b1():
            nc.vector.tensor_scalar_mul(
                out=b1_all[:].rearrange("p (t m) -> p t m", t=PACK),
                in0=kept["b1_ps"][:].rearrange("p (m t) -> p t m", t=PACK),
                scalar1=1.0 / H,
            )

        def warm_up():
            waste = psum_x1.tile([P, H], F32, tag="x1_ps", name="waste")
            for turn in range(4):
                nc.tensor.matmul(out=waste[:], lhsT=ones[:], rhs=blank[:], start=True, stop=True)

        def widen_vectors():
            nc.gpsimd.tensor_copy(out=gamma_cols[:], in_=gamma_bf[:])
            nc.gpsimd.tensor_copy(out=beta_cols[:], in_=beta_bf[:])

        def spread_b2():
            b2_ps = psum_z.tile([P, G], F32, tag="zT")
            nc.tensor.matmul(out=b2_ps[:], lhsT=ones[:], rhs=b2_row[:], start=True, stop=True)
            nc.scalar.copy(out=b2_all[:], in_=b2_ps[:])

        def gpsimd_group(grouped, planes):
            nc.gpsimd.tensor_scalar(
                out=grouped,
                in0=planes.rearrange("p t c -> p c t"),
                scalar1=1.0,
                scalar2=0.0,
                op0=ALU.mult,
                op1=ALU.add,
            )


        def transpose_x(unit, tiles=range(TILES), pool=psum_x, tag="xT"):
            x_words = x_sb[unit][:].bitcast(F32)
            if tiles[0] == 0:
                kept["xT", unit] = pool.tile([P, TILES, 2, P], F32, tag=tag, name="xT")
            xT = kept["xT", unit]
            for i in tiles:
                for u in range(2):
                    nc.tensor.transpose(
                        out=xT[:, i, u, :],
                        in_=x_words[:, WORDS * i + u : WORDS * (i + 1) : 2],
                        identity=ident[:],
                    )

        def columns(tiles):
            return slice(tiles[0] * P, (tiles[-1] + 1) * P)

        def group_x(unit, tiles=range(TILES)):
            if unit in shared_x:
                kept["x_grouped", unit] = mixed[:, X_PLACE[unit % 2] : X_PLACE[unit % 2] + UNIT, :]
            elif tiles[0] == 0:
                x_grouped = four.tile([P, UNIT, PACK], BF16, align_bytes=64)
                kept["x_grouped", unit] = x_grouped[:]
            nc.scalar.copy(
                out=kept["x_grouped", unit]
                .rearrange("p c t -> p (c t)")
                .bitcast(F32)
                .rearrange("p (i c u) -> p i c u", i=TILES, u=2)[:, tiles[0] : tiles[-1] + 1, :, :],
                in_=kept["xT", unit][:, tiles[0] : tiles[-1] + 1, :, :].rearrange("p i u c -> p i c u"),
            )

        def quantise_x(unit, tiles=range(TILES)):
            if tiles[0] == 0:
                x_codes = four.tile([P, UNIT], U32, align_bytes=64)
                x_scales = four.tile([P, UNIT], U8, align_bytes=64)
                kept["x_codes", unit] = x_codes[:]
                kept["x_scales", unit] = x_scales[:]
            quantise(
                nc,
                kept["x_codes", unit][:, columns(tiles)],
                kept["x_scales", unit][:, columns(tiles)],
                kept["x_grouped", unit][:, columns(tiles), :],
            )

        def multiply_w1(unit):
            for i in range(TILES):
                h_ps = psum_h.tile([P, H], F32, tag="h_ps")
                nc.tensor.matmul_mx(
                    out=h_ps[:],
                    lhsT=kept["x_codes", unit][:, i * P : (i + 1) * P].bitcast(FP8X4),
                    lhsT_scale=kept["x_scales", unit][:, i * P : (i + 1) * P],
                    rhs=w1_codes[:].bitcast(FP8X4),
                    rhs_scale=w1_scales[:],
                    start=True,
                    stop=True,
                )
                kept["h_ps", unit, i] = h_ps

        def add_b1(unit):
            h = every.tile([P, TILES, H], F32)
            mean = every.tile([P, TILES], F32)
            for i in range(TILES):
                nc.vector.scalar_tensor_tensor(
                    out=h[:, i, :],
                    in0=kept["h_ps", unit, i][:],
                    scalar=1.0 / H,
                    in1=b1_all[:],
                    op0=ALU.mult,
                    op1=ALU.add,
                    accum_out=mean[:, i : i + 1],
                )
            kept["h", unit] = h
            kept["mean", unit] = mean

        def sum_squares(unit):
            sq_sum = every.tile([P, TILES], F32)
            for i in range(TILES):
                squares = four.tile([P, H], BF16)
                nc.scalar.activation(
                    out=squares[:],
                    in_=kept["h", unit][:, i, :],
                    func=ACT.Square,
                    bias=kept["mean", unit][:, i : i + 1],
                    scale=-float(H),
                    accum_out=sq_sum[:, i : i + 1],
                )
            kept["sq_sum", unit] = sq_sum

        def take_root(unit):
            inv_std = every.tile([P, TILES], F32)
            nc.scalar.activation(
                out=inv_std[:],
                in_=kept["sq_sum", unit][:],
                func=ACT.Abs_reciprocal_sqrt,
                bias=eps_col[:],
                scale=1.0 / H**3,
            )
            kept["inv_std", unit] = inv_std

        def scale_mean(unit):
            small_mean = every.tile([P, TILES], F32)
            nc.scalar.mul(out=small_mean[:], in_=kept["mean", unit][:], mul=1.0 / H)
            kept["small_mean", unit] = small_mean

        def normalise(unit):
            z = four.tile([P, TILES, H], F32)
            for i in range(TILES):
                nc.vector.tensor_scalar(
                    out=z[:, i, :],
                    in0=kept["h", unit][:, i, :],
                    scalar1=kept["small_mean", unit][:, i : i + 1],
                    scalar2=kept["inv_std", unit][:, i : i + 1],
                    op0=ALU.subtract,
                    op1=ALU.mult,
                )
            kept["z", unit] = z

        def transpose_z(unit):
            for bank in range(2):
                pool, tag = (psum_h, "h_ps") if unit >= UNITS - 2 else (psum_z, "zT")
                zT = pool.tile([P, 2, UNIT], F32, tag=tag, name="zT")
                for s in range(2):
                    t = 2 * bank + s
                    for i in range(TILES):
                        nc.tensor.transpose(
                            out=zT[:, s, i * P : (i + 1) * P],
                            in_=kept["z", unit][:, i, t * P : (t + 1) * P],
                            identity=ident[:],
                        )
                kept["zT", unit, bank] = zT

        def scale_relu(unit):
            r_planes = every.tile([P, H_CHUNKS, UNIT], BF16)
            for t in (1, 0, 3, 2):
                nc.scalar.activation(
                    out=r_planes[:, t, :],
                    in_=kept["zT", unit, t // 2][:, t % 2, :],
                    func=ACT.Relu,
                    bias=beta_cols[:, t : t + 1],
                    scale=gamma_cols[:, t : t + 1],
                )
            kept["r_planes", unit] = r_planes[:]

        def group_r(unit):
            if unit in shared_r:
                r_grouped = mixed[:, R_PLACE : R_PLACE + UNIT, :]
            else:
                r_alone = two.tile([P, UNIT, PACK], BF16, align_bytes=64)
                r_grouped = r_alone[:]
            if unit == UNITS - 1:
                for copy, part in ((nc.scalar.copy, columns([0])), (nc.vector.tensor_copy, columns([1]))):
                    group_words(copy, r_grouped[:, part, :], kept["r_planes", unit][:, :, part])
            elif unit >= UNITS - VECTOR_GROUPS:
                group_words(nc.vector.tensor_copy, r_grouped, kept["r_planes", unit])
            else:
                gpsimd_group(r_grouped, kept["r_planes", unit])
            kept["r_grouped", unit] = r_grouped

        def quantise_r(unit):
            r_codes = four.tile([P, UNIT], U32, align_bytes=64)
            r_scales = four.tile([P, UNIT], U8, align_bytes=64)
            quantise(nc, r_codes[:], r_scales[:], kept["r_grouped", unit])
            kept["r_codes", unit] = r_codes[:]
            kept["r_scales", unit] = r_scales[:]

        def quantise_both(unit):
            x_unit = unit + R_LAG + X_AHEAD
            codes = four.tile([P, 2 * UNIT], U32, align_bytes=64)
            scales = four.tile([P, 2 * UNIT], U8, align_bytes=64)
            first = min(R_PLACE, X_PLACE[x_unit % 2])
            quantise(nc, codes[:], scales[:], mixed[:, first : first + 2 * UNIT, :])
            x_part = slice(X_PLACE[x_unit % 2] - first, X_PLACE[x_unit % 2] - first + UNIT)
            r_part = slice(R_PLACE - first, R_PLACE - first + UNIT)
            kept["x_codes", x_unit] = codes[:, x_part]
            kept["x_scales", x_unit] = scales[:, x_part]
            kept["r_codes", unit] = codes[:, r_part]
            kept["r_scales", unit] = scales[:, r_part]

        def multiply_w2(unit):
            pool, tag = (psum_x, "xT") if unit in X_BANK_X1 else (psum_x1, "x1_ps")
            x1_ps = pool.tile([P, G_CHUNKS, UNIT], F32, tag=tag, name="x1_ps")
            x1 = [x1_ps[:, c, :] for c in range(G_CHUNKS)]
            if unit == UNITS - 1:
                x1_late = psum_z.tile([P, UNIT], F32, tag="zT", name="x1_late")
                x1[1] = x1_late[:]
            for c in range(G_CHUNKS) if unit == UNITS - 1 else (0, 1, 0, 1):
                nc.tensor.matmul_mx(
                    out=x1[c],
                    lhsT=w2_codes[:, c * P : (c + 1) * P].bitcast(FP8X4),
                    lhsT_scale=w2_scales[:, c * P : (c + 1) * P],
                    rhs=kept["r_codes", unit].bitcast(FP8X4),
                    rhs_scale=kept["r_scales", unit],
                    start=True,
                    stop=True,
                )
            kept["x1_ps", unit] = x1_ps
            kept["x1", unit] = x1

        def take_max(unit):
            lines = slice(unit * LINES_PER_UNIT, (unit + 1) * LINES_PER_UNIT)
            if unit == UNITS - 1:
                for c in range(G_CHUNKS):
                    nc.vector.tensor_reduce(
                        out=best[:, c, lines],
                        in_=kept["x1", unit][c].rearrange("m (b l) -> m b l", l=NODES),
                        axis=AXIS.X,
                        op=ALU.max,
                    )
            else:
                nc.vector.tensor_reduce(
                    out=best[:, :, lines],
                    in_=kept["x1_ps", unit][:].rearrange("m c (b l) -> m c b l", l=NODES),
                    axis=AXIS.X,
                    op=ALU.max,
                )

        def at(step, unit):
            if 0 <= unit < UNITS:
                step(unit)

        warm_up()
        for i in range(TILES):
            transpose_x(0, [i])
        spread_b1()
        transpose_x(1, pool=psum_z, tag="zT")
        group_x(0, [0])
        group_w1()
        group_x(0, [1])
        group_x(1)
        transpose_x(2)
        group_x(2)
        transpose_x(3, pool=psum_z, tag="zT")
        quantise_x(0, [0])
        quantise(nc, w1_codes[:], w1_scales[:], w1_grouped[:])
        quantise_x(0, [1])
        place_b1()
        quantise_x(1)
        multiply_w1(0)
        for now in range(1, UNITS + LAST_LAG):
            at(sum_squares, now - 2)
            at(group_x, now + X_AHEAD + 1)
            at(scale_mean, now - 2)
            at(take_root, now - 2)
            if now < UNITS + 1:
                at(group_r, now - 5)
            at(add_b1, now - 1)
            if now < UNITS + 1:
                at(take_max, now - 7)
                if now + X_AHEAD not in shared_x:
                    at(quantise_x, now + X_AHEAD)
                at(normalise, now - 3)
            else:
                at(normalise, now - 3)
                at(group_r, now - 5)
                at(take_max, now - 7)
            at(transpose_z, now - 4)
            at(scale_relu, now - 4)
            if now - R_LAG in shared_r:
                quantise_both(now - R_LAG)
            else:
                at(quantise_r, now - R_LAG)
            at(multiply_w1, now)
            at(transpose_x, now + X_AHEAD + 2)
            at(multiply_w2, now - 6)
            if now == 3:
                widen_vectors()
            if now == 4:
                group_words(nc.vector.tensor_copy, w2_grouped[:], w2_raw[:])
            if now == 5:
                quantise(nc, w2_codes[:], w2_scales[:], w2_grouped[:])
            if now == UNITS + 3:
                spread_b2()

        out_sb = const.tile([P, G_CHUNKS, P], F32)
        for c in range(G_CHUNKS):
            outT = psum_h.tile([P, P], F32, tag="h_ps", name="outT")
            nc.tensor.transpose(out=outT[:], in_=best[:, c, :], identity=ident[:])
            nc.vector.tensor_add(out=out_sb[:, c, :], in0=outT[:], in1=b2_all[:, c * P : (c + 1) * P])
            for half, queue in enumerate((nc.sync, nc.scalar)):
                first = half * G + c * P
                queue.dma_start(out=out[:, first : first + P], in_=out_sb[0:POLYLINES, c, :])
